import numpy as np
import ml_dtypes


def mxq(x, axis, fmt="e4m3"):
    dtype, down = {"e4m3": (ml_dtypes.float8_e4m3fn, 7), "e5m2": (ml_dtypes.float8_e5m2, 14)}[fmt]
    v = np.moveaxis(np.asarray(x, np.float32).astype(ml_dtypes.bfloat16).astype(np.float64), axis, -1)
    blocks = v.reshape(v.shape[:-1] + (-1, 32))
    amax = np.abs(blocks).max(-1, keepdims=True)
    byte = np.maximum(np.where(amax > 0, np.frexp(amax)[1] - 1 + 127, 0) - down, 1)
    scale = np.exp2(byte - 127.0)
    codes = (blocks / scale).astype(np.float32).astype(dtype).astype(np.float64)
    return np.moveaxis((codes * scale).reshape(v.shape), -1, axis)


WIDE = False


def mx_kscale(k):
    if not WIDE:
        return np.ones(k)
    levels = np.array([10, -10, 5, -5, 0])
    if k % 512:
        return np.exp2(np.random.permutation(np.resize(levels, k // 32))).repeat(32)
    a = np.empty((k // 512, 16))
    for p in range(k // 512):
        a[p, :8] = np.random.permutation(np.resize(levels, 8))
        for g in range(8):
            far = levels[np.abs(levels - a[p, g]) >= 10]
            a[p, g + 8] = far[np.random.randint(len(far))]
    return np.exp2(a.ravel()).repeat(32)


BF16 = ml_dtypes.bfloat16


def bf(x):
    return np.asarray(x, np.float32).astype(BF16)


def f64(x):
    return np.asarray(x).astype(np.float64)


B, S, E, H, KV, DH = 4, 1024, 1024, 4, 1, 128
THETA = 10000.0


def rope(x):
    b, s, h, hd = x.shape
    half = hd // 2
    inv_freq = 1.0 / THETA ** (f64(np.arange(0, half, 2)) / half)
    pos = np.broadcast_to(f64(np.arange(s))[None, :], (b, s))
    freqs = pos[:, :, None] * inv_freq[None, None, :]
    cos = np.cos(freqs)[:, :, None, :]
    sin = np.sin(freqs)[:, :, None, :]
    pairs = x[..., :half].reshape(b, s, h, half // 2, 2)
    x0, x1 = pairs[..., 0], pairs[..., 1]
    rot = np.stack([x0 * cos - x1 * sin, x0 * sin + x1 * cos], axis=-1).reshape(b, s, h, half)
    return np.concatenate([rot, x[..., half:]], axis=-1)


def setup_inputs():
    s = mx_kscale(E)
    return {"hidden_states": bf(np.random.standard_normal((B, S, E)) * s),
            "Wq": bf(np.random.standard_normal((E, H * DH)) * 1.25 / np.sqrt(E) / s[:, None]),
            "Wk": bf(np.random.standard_normal((E, KV * DH)) * 1.25 / np.sqrt(E) / s[:, None]),
            "Wv": bf(np.random.standard_normal((E, KV * DH)) * 1.25 / np.sqrt(E) / s[:, None])}


def reference(hidden_states, Wq, Wk, Wv):
    xq = mxq(f64(hidden_states), 2, "e4m3")
    q = (xq @ mxq(f64(Wq), 0, "e4m3")).reshape(B, S, H, DH)
    k = (xq @ mxq(f64(Wk), 0, "e4m3")).reshape(B, S, KV, DH)
    v = (xq @ mxq(f64(Wv), 0, "e4m3")).reshape(B, S, KV, DH)
    return rope(q), rope(k), v

@@ -1,0 +1,402 @@
+import math
+from contextlib import ExitStack
+
+import concourse.mybir as mybir
+from concourse.masks import make_identity
+
+FLOPS = 2 * 4096 * 1024 * 768
+
+F32 = mybir.dt.float32
+BF16 = mybir.dt.bfloat16
+I32 = mybir.dt.int32
+U32 = mybir.dt.uint32
+U8 = mybir.dt.uint8
+FP8X4 = mybir.dt.float8_e4m3fn_x4
+ALU = mybir.AluOpType
+ACT = mybir.ActivationFunctionType
+
+P = 128
+NB = 4
+TPP = 8
+E = 1024
+NPAIR = 16
+THETA = 10000.0
+TWO_PI = 2.0 * math.pi
+C1 = 51472.0 / 8192.0
+C2 = TWO_PI - C1
+
+X_CHUNKS = [(0, 0, 2), (0, 2, 2), (0, 4, 4), (1, 0, 4), (1, 4, 4), (2, 0, 4), (2, 4, 4), (3, 0, 4), (3, 4, 4)]
+Q_GROUPS = [[0, 1], [2, 3], [4, 5], [6, 7], [8, 9], [10, 11], [12, 13], [14], [15]]
+KV_GROUPS = [[0, 1, 2, 3], [4, 5, 6, 7], [8, 9, 10, 11], [12, 13], [14], [15]]
+
+
+def tile_diffucoderattention_pa_t_kernel(tc, hidden_states, Wq, Wk, Wv, out_0, out_1, out_2):
+    nc = tc.nc
+    with ExitStack() as ctx:
+        const = ctx.enter_context(tc.tile_pool(name="const", bufs=1))
+        xin = ctx.enter_context(tc.tile_pool(name="xin", bufs=1))
+        work = ctx.enter_context(tc.tile_pool(name="work", bufs=4))
+        rope = ctx.enter_context(tc.tile_pool(name="rope", bufs=3))
+        outp = ctx.enter_context(tc.tile_pool(name="outp", bufs=4))
+        psum = ctx.enter_context(tc.psum_pool(name="psum", bufs=2))
+        ctx.enter_context(tc.manual_schedule())
+
+        wq_raw = [const.tile([P, 2048], BF16, name="wq_raw%d" % g) for g in range(2)]
+        wk_raw = const.tile([P, 1024], BF16, name="wk_raw")
+        wv_raw = const.tile([P, 1024], BF16, name="wv_raw")
+        wq_view = Wq.rearrange("(g q t) c -> g q (t c)", g=2, q=P, t=4)
+        for g in range(2):
+            nc.sync.dma_start(out=wq_raw[g][:], in_=wq_view[g])
+        x_tiles = []
+        x_of_pair = {}
+        for ci, (b, j0, nj) in enumerate(X_CHUNKS):
+            xt = xin.tile([P, nj * E], BF16, name="x%d" % ci)
+            x_tiles.append(xt)
+            for k in range(nj // 2):
+                x_of_pair[b * 4 + j0 // 2 + k] = (xt, 2 * k)
+
+        def load_x(ci):
+            b, j0, nj = X_CHUNKS[ci]
+            src = hidden_states[b].rearrange("(p j) e -> p (j e)", j=TPP)
+            nc.sync.dma_start(out=x_tiles[ci][:], in_=src[:, j0 * E : (j0 + nj) * E])
+
+        load_x(0)
+        load_x(1)
+        nc.sync.dma_start(
+            out=wk_raw[:].rearrange("p (g x) -> p g x", g=2),
+            in_=Wk.rearrange("(g q t) c -> q g (t c)", g=2, q=P, t=4),
+        )
+        nc.sync.dma_start(
+            out=wv_raw[:].rearrange("p (g x) -> p g x", g=2),
+            in_=Wv.rearrange("(g q t) c -> q g (t c)", g=2, q=P, t=4),
+        )
+        for ci in range(2, len(X_CHUNKS)):
+            load_x(ci)
+
+        pos_i = const.tile([P, TPP], I32, name="pos_i")
+        nc.gpsimd.iota(pos_i[:], pattern=[[1, TPP]], base=0, channel_multiplier=TPP)
+        ident = const.tile([P, P], F32, name="ident")
+        make_identity(nc, ident[:])
+
+        zero1 = const.tile([P, 1], F32, name="zero1")
+        warm = const.tile([P, 1], F32, name="warm")
+        nc.vector.memset(zero1[:], 0.0)
+        nc.scalar.activation(out=warm[:], in_=zero1[:], func=ACT.Sin)
+
+        NT = TPP * 32
+        pos_f = const.tile([P, TPP], F32, name="pos_f")
+        freq = const.tile([P, 32], F32, name="freq")
+        ang = const.tile([P, NT], F32, name="ang")
+        turns_i = const.tile([P, NT], I32, name="turns_i")
+        turns = const.tile([P, NT], F32, name="turns")
+        red1 = const.tile([P, NT], F32, name="red1")
+        red = const.tile([P, NT], F32, name="red")
+        nabs = const.tile([P, NT], F32, name="nabs")
+        carg = const.tile([P, NT], F32, name="carg")
+        sin_h = const.tile([P, NT], F32, name="sin_h")
+        cos_h = const.tile([P, NT], F32, name="cos_h")
+        sq_h = const.tile([P, NT], F32, name="sq_h")
+        sin_half = const.tile([P, NT], F32, name="sin_half")
+        sign2 = const.tile([P, 2], F32, name="sign2")
+        tab = const.tile([P, 4, 2, 2, 64], F32, name="tab")
+
+        nc.vector.tensor_copy(out=pos_f[:], in_=pos_i[:])
+        nc.vector.memset(freq[:, 0:1], 1.0)
+        nc.vector.memset(sign2[:, 0:1], 2.0)
+        nc.vector.memset(sign2[:, 1:2], -2.0)
+        w = 1
+        while w < 32:
+            nc.vector.tensor_scalar(
+                out=freq[:, w : 2 * w], in0=freq[:, 0:w], scalar1=THETA ** (-w / 32.0), scalar2=None, op0=ALU.mult
+            )
+            w *= 2
+        nc.vector.tensor_tensor(
+            out=ang[:].rearrange("p (j i) -> p j i", j=TPP),
+            in0=pos_f[:].unsqueeze(2).to_broadcast([P, TPP, 32]),
+            in1=freq[:].unsqueeze(1).to_broadcast([P, TPP, 32]),
+            op=ALU.mult,
+        )
+        nc.vector.tensor_scalar(
+            out=turns_i[:], in0=ang[:], scalar1=1.0 / TWO_PI, scalar2=0.25, op0=ALU.mult, op1=ALU.add
+        )
+        nc.vector.tensor_copy(out=turns[:], in_=turns_i[:])
+        nc.vector.scalar_tensor_tensor(out=red1[:], in0=turns[:], scalar=-C1, in1=ang[:], op0=ALU.mult, op1=ALU.add)
+        nc.vector.scalar_tensor_tensor(out=red[:], in0=turns[:], scalar=-C2, in1=red1[:], op0=ALU.mult, op1=ALU.add)
+        nc.vector.scalar_tensor_tensor(out=nabs[:], in0=red[:], scalar=-1.0, in1=red[:], op0=ALU.mult, op1=ALU.min)
+        nc.vector.tensor_scalar(
+            out=carg[:], in0=nabs[:], scalar1=0.5, scalar2=0.5 * math.pi, op0=ALU.mult, op1=ALU.add
+        )
+        nc.scalar.activation(out=sin_h[:], in_=red[:], func=ACT.Sin, scale=0.5)
+        nc.scalar.activation(out=cos_h[:], in_=carg[:], func=ACT.Sin)
+        nc.scalar.activation(out=sq_h[:], in_=sin_h[:], func=ACT.Square)
+
+        def transposes(n):
+            xt, off = x_of_pair[n]
+            xw = xt[:].bitcast(F32)
+            banks = []
+            for a in range(2):
+                tp = psum.tile([P, 4, P], F32, name="tp%d" % a, tag="tp%d" % a, bufs=1)
+                for v in range(4):
+                    c0 = (off + a) * 512 + (v // 2) * 256 + v % 2
+                    nc.tensor.transpose(tp[:, v, :], xw[:, c0 : c0 + 255 : 2], ident[:])
+                banks.append(tp)
+            return banks
+
+        def evacuate(banks):
+            xg = work.tile([P, 2048], BF16, name="xg", tag="xg", align_bytes=64)
+            xgw = xg[:].bitcast(F32).rearrange("p (a g r u) -> p a g r u", a=2, g=2, r=P, u=2)
+            for a in range(2):
+                nc.scalar.copy(out=xgw[:, a], in_=banks[a][:].rearrange("p (g u) r -> p g r u", u=2))
+            return xg
+
+        def quantise_x(xg):
+            xc = work.tile([P, 512], U32, name="xc", tag="xc", align_bytes=64)
+            xs = work.tile([P, 512], U8, name="xs", tag="xs", align_bytes=64)
+            nc.vector.quantize_mx(out=xc[:].bitcast(FP8X4), scales=xs[:], in_=xg[:])
+            return xc, xs
+
+        xg_of = {}
+        xq_of = {}
+
+        wg = const.tile([P, 2 * 768 * 4], BF16, name="wg", align_bytes=64)
+        wg_v = wg[:].rearrange("p (g c t) -> p g c t", g=2, c=768, t=4)
+        wc = const.tile([P, 2, 768], U32, name="wc", align_bytes=64)
+        ws = const.tile([P, 2, 768], U8, name="ws", align_bytes=64)
+
+        def regroup_q(copy, g, s):
+            src = wq_raw[g][:].rearrange("p (t h s f) -> p s h f t", t=4, h=4, s=2, f=64)
+            copy(out=wg_v[:, g, s * 256 : (s + 1) * 256, :].rearrange("p (h f) t -> p h f t", h=4), in_=src[:, s])
+
+        def regroup_kv(raw, c0):
+            nc.vector.tensor_copy(
+                out=wg_v[:, :, c0 : c0 + P, :], in_=raw[:].rearrange("p (g t c) -> p g c t", g=2, t=4, c=P)
+            )
+
+        def quantise_w(g, c0, c1):
+            nc.vector.quantize_mx(
+                out=wc[:, g, c0:c1].bitcast(FP8X4),
+                scales=ws[:, g, c0:c1],
+                in_=wg_v[:, g, c0:c1, :].rearrange("p c t -> p (c t)"),
+            )
+
+        regroup_q(nc.vector.tensor_copy, 0, 0)
+        regroup_q(nc.scalar.copy, 0, 1)
+        nc.vector.tensor_tensor(out=sin_half[:], in0=sin_h[:], in1=cos_h[:], op=ALU.mult)
+        regroup_q(nc.vector.tensor_copy, 1, 0)
+        regroup_q(nc.scalar.copy, 1, 1)
+        xg_of[0] = evacuate(transposes(0))
+        xg_of[1] = evacuate(transposes(1))
+        quantise_w(0, 0, 256)
+        quantise_w(1, 0, 256)
+        quantise_w(0, 256, 512)
+        quantise_w(1, 256, 512)
+        nc.vector.tensor_tensor(
+            out=tab[:, :, 1].rearrange("p q a (i e) -> p q (a i) e", e=2),
+            in0=sin_half[:].rearrange("p (q x) -> p q x", q=4).unsqueeze(3).to_broadcast([P, 4, 64, 2]),
+            in1=sign2[:].unsqueeze(1).unsqueeze(1).to_broadcast([P, 4, 64, 2]),
+            op=ALU.mult,
+        )
+        xq_of[0] = quantise_x(xg_of[0])
+        regroup_kv(wk_raw, 512)
+        xq_of[1] = quantise_x(xg_of[1])
+        regroup_kv(wv_raw, 640)
+        quantise_w(0, 512, 768)
+        quantise_w(1, 512, 768)
+        nc.vector.tensor_scalar(
+            out=tab[:, :, 0].rearrange("p q a (i e) -> p q (a i) e", e=2),
+            in0=sq_h[:].rearrange("p (q x) -> p q x", q=4).unsqueeze(3).to_broadcast([P, 4, 64, 2]),
+            scalar1=-2.0,
+            scalar2=1.0,
+            op0=ALU.mult,
+            op1=ALU.add,
+        )
+
+        banks_of = {}
+        q_tile_of = {}
+        kv_tile_of = {}
+
+        def mx(n, bank, c0):
+            xc, xs = xq_of[n]
+            for a in range(2):
+                for g in range(2):
+                    blk = slice((a * 2 + g) * P, (a * 2 + g + 1) * P)
+                    nc.tensor.matmul_mx(
+                        out=bank[:, a * 256 : (a + 1) * 256],
+                        lhsT=xc[:, blk].bitcast(FP8X4),
+                        lhsT_scale=xs[:, blk],
+                        rhs=wc[:, g, c0 : c0 + 256].bitcast(FP8X4),
+                        rhs_scale=ws[:, g, c0 : c0 + 256],
+                        start=(g == 0),
+                        stop=(g == 1),
+                    )
+
+        def out_tiles(n):
+            for grp in Q_GROUPS:
+                if grp[0] == n:
+                    qo = outp.tile([P, len(grp) * 8, P], F32, name="qo", tag="qo")
+                    for k, m in enumerate(grp):
+                        q_tile_of[m] = (qo, k, grp)
+            for grp in KV_GROUPS:
+                if grp[0] == n:
+                    ko = outp.tile([P, len(grp) * 2, P], F32, name="ko", tag="ko", bufs=3)
+                    vo = outp.tile([P, len(grp) * 2, P], F32, name="vo", tag="vo", bufs=3)
+                    for k, m in enumerate(grp):
+                        kv_tile_of[m] = (ko, vo, k, grp)
+
+        rope_tmp = {}
+
+        def rope_q_mul(n):
+            t12 = rope.tile([P, 2, 512], F32, name="t12q", tag="t12q")
+            nc.vector.tensor_tensor(
+                out=t12[:].rearrange("p c (a h f) -> p c a h f", a=2, h=4),
+                in0=banks_of[n][0][:]
+                .rearrange("p (a h f) -> p a h f", a=2, h=4)
+                .unsqueeze(1)
+                .to_broadcast([P, 2, 2, 4, 64]),
+                in1=tab[:, n % 4].unsqueeze(3).to_broadcast([P, 2, 2, 4, 64]),
+                op=ALU.mult,
+            )
+            rope_tmp[("q", n)] = t12
+
+        def rope_q_add(n, eng, m0=0, m1=8):
+            qo, k, grp = q_tile_of[n]
+            t12 = rope_tmp[("q", n)]
+            eng.tensor_tensor(
+                out=qo[:, 8 * k + m0 : 8 * k + m1, 0:64].rearrange("p m (i e) -> p m i e", e=2),
+                in0=t12[:, 0].rearrange("p (m i e) -> p m i e", m=8, e=2)[:, m0:m1],
+                in1=t12[:, 1].rearrange("p (m i e) -> p m i e", m=8, e=2)[:, m0:m1, :, ::-1],
+                op=ALU.add,
+            )
+
+        def store_q_tile(n, a):
+            qo, k, grp = q_tile_of[n]
+            b, j = n // 4, 2 * (n % 4) + a
+            dst = out_0[b].rearrange("(p j) h d -> p (j h d)", j=TPP)
+            nc.sync.dma_start(
+                out=dst[:, j * 512 : (j + 1) * 512],
+                in_=qo[:, 8 * k + 4 * a : 8 * k + 4 * a + 4, :].rearrange("p m d -> p (m d)"),
+            )
+
+        def rope_k_mul(n):
+            t12 = rope.tile([P, 2, 2, 64], F32, name="t12k", tag="t12k")
+            nc.vector.tensor_tensor(
+                out=t12[:],
+                in0=banks_of[n][2][:]
+                .rearrange("p (a s f) -> p a s f", a=2, s=4)[:, :, 0, :]
+                .unsqueeze(1)
+                .to_broadcast([P, 2, 2, 64]),
+                in1=tab[:, n % 4],
+                op=ALU.mult,
+            )
+            rope_tmp[("k", n)] = t12
+            ko, vo, k, grp = kv_tile_of[n]
+            nc.vector.tensor_copy(
+                out=ko[:, 2 * k : 2 * k + 2, 64:128],
+                in_=banks_of[n][2][:].rearrange("p (a s f) -> p a s f", a=2, s=4)[:, :, 1, :],
+            )
+
+        def rope_k_add(n):
+            ko, vo, k, grp = kv_tile_of[n]
+            t12 = rope_tmp[("k", n)]
+            nc.vector.tensor_tensor(
+                out=ko[:, 2 * k : 2 * k + 2, 0:64].rearrange("p a (i e) -> p a i e", e=2),
+                in0=t12[:, 0].rearrange("p a (i e) -> p a i e", e=2),
+                in1=t12[:, 1].rearrange("p a (i e) -> p a i e", e=2)[:, :, :, ::-1],
+                op=ALU.add,
+            )
+
+        def copy_q(n):
+            qo, k, grp = q_tile_of[n]
+            nc.scalar.copy(
+                out=qo[:, 8 * k : 8 * k + 8, 64:128], in_=banks_of[n][1][:].rearrange("p (m f) -> p m f", m=8)
+            )
+
+        def copy_kv(n):
+            bank_k = banks_of[n][2]
+            ko, vo, k, grp = kv_tile_of[n]
+            nc.scalar.copy(
+                out=vo[:, 2 * k : 2 * k + 2, :], in_=bank_k[:].rearrange("p (a s f) -> p a s f", a=2, s=2)[:, :, 1, :]
+            )
+
+        def store_q(n):
+            qo, k, grp = q_tile_of[n]
+            if grp[-1] != n:
+                return
+            b, j0 = grp[0] // 4, 2 * (grp[0] % 4)
+            dst = out_0[b].rearrange("(p j) h d -> p (j h d)", j=TPP)
+            nc.sync.dma_start(
+                out=dst[:, j0 * 512 : (j0 + 2 * len(grp)) * 512], in_=qo[:].rearrange("p m d -> p (m d)")
+            )
+
+        def store_kv(n):
+            ko, vo, k, grp = kv_tile_of[n]
+            if grp[-1] != n:
+                return
+            b, j0 = grp[0] // 4, 2 * (grp[0] % 4)
+            for dram, sb in ((out_1, ko), (out_2, vo)):
+                dst = dram[b].rearrange("(p j) o d -> p (j o d)", j=TPP)
+                nc.sync.dma_start(
+                    out=dst[:, j0 * P : (j0 + 2 * len(grp)) * P], in_=sb[:].rearrange("p m d -> p (m d)")
+                )
+
+        def new_banks(n):
+            out_tiles(n)
+            bank_r = psum.tile([P, 512], F32, name="bank_r", tag="bank_r")
+            bank_p = psum.tile([P, 512], F32, name="bank_p", tag="bank_p")
+            bank_k = psum.tile([P, 512], F32, name="bank_k", tag="bank_k")
+            banks_of[n] = (bank_r, bank_p, bank_k)
+
+        def mx_q(n):
+            mx(n, banks_of[n][0], 0)
+            mx(n, banks_of[n][1], 256)
+            copy_q(n)
+
+        def mx_kv(n):
+            mx(n, banks_of[n][2], 512)
+            copy_kv(n)
+
+        def ahead(n):
+            if n < NPAIR:
+                xg_of[n] = evacuate(transposes(n))
+
+        def vector_part(n):
+            rope_q_mul(n)
+            rope_q_add(n, nc.gpsimd)
+            store_q(n)
+            if n + 2 < NPAIR:
+                xq_of[n + 2] = quantise_x(xg_of[n + 2])
+            if n > 0:
+                rope_k_add(n - 1)
+                store_kv(n - 1)
+            rope_k_mul(n)
+
+        new_banks(0)
+        new_banks(1)
+        mx_q(0)
+        mx_q(1)
+        ahead(2)
+        mx_kv(0)
+        mx_kv(1)
+        ahead(3)
+        vector_part(0)
+        vector_part(1)
+        for n in range(2, NPAIR - 1):
+            new_banks(n)
+            mx_q(n)
+            ahead(n + 2)
+            mx_kv(n)
+            vector_part(n)
+
+        last = NPAIR - 1
+        new_banks(last)
+        mx_kv(last)
+        mx_q(last)
+        rope_k_add(last - 1)
+        store_kv(last - 1)
+        rope_k_mul(last)
+        rope_k_add(last)
+        store_kv(last)
+        rope_q_mul(last)
+        for a in range(2):
+            rope_q_add(last, nc.vector, 4 * a, 4 * a + 4)
+            store_q_tile(last, a)

@@ -25,9 +25,11 @@ TWO_PI = 2.0 * math.pi
 C1 = 51472.0 / 8192.0
 C2 = TWO_PI - C1
 
-X_CHUNKS = [(0, 0, 2), (0, 2, 2), (0, 4, 4), (1, 0, 4), (1, 4, 4), (2, 0, 4), (2, 4, 4), (3, 0, 4), (3, 4, 4)]
-Q_GROUPS = [[0, 1], [2, 3], [4, 5], [6, 7], [8, 9], [10, 11], [12, 13], [14], [15]]
-KV_GROUPS = [[0, 1, 2, 3], [4, 5, 6, 7], [8, 9, 10, 11], [12, 13], [14], [15]]
+X_CHUNKS = [(0, 0, 2), (0, 2, 2), (0, 4, 2), (0, 6, 2), (1, 0, 4), (1, 4, 4), (2, 0, 4), (2, 4, 4), (3, 0, 4), (3, 4, 4)]
+K_LAG = 2
+T_AHEAD = 3
+Q_GROUPS = [[0, 1], [2, 3], [4, 5], [6, 7], [8, 9], [10], [11], [12], [13], [14], [15]]
+KV_GROUPS = [[0, 1], [2, 3], [4, 5], [6, 7], [8, 9], [10, 11], [12], [13], [14], [15]]
 
 
 def tile_diffucoderattention_pa_t_kernel(tc, hidden_states, Wq, Wk, Wv, out_0, out_1, out_2):
@@ -45,8 +47,6 @@ def tile_diffucoderattention_pa_t_kernel(tc, hidden_states, Wq, Wk, Wv, out_0, o
         wk_raw = const.tile([P, 1024], BF16, name="wk_raw")
         wv_raw = const.tile([P, 1024], BF16, name="wv_raw")
         wq_view = Wq.rearrange("(g q t) c -> g q (t c)", g=2, q=P, t=4)
-        for g in range(2):
-            nc.sync.dma_start(out=wq_raw[g][:], in_=wq_view[g])
         x_tiles = []
         x_of_pair = {}
         for ci, (b, j0, nj) in enumerate(X_CHUNKS):
@@ -61,7 +61,11 @@ def tile_diffucoderattention_pa_t_kernel(tc, hidden_states, Wq, Wk, Wv, out_0, o
             nc.sync.dma_start(out=x_tiles[ci][:], in_=src[:, j0 * E : (j0 + nj) * E])
 
         load_x(0)
+        for g in range(2):
+            nc.sync.dma_start(out=wq_raw[g][:], in_=wq_view[g])
         load_x(1)
+        load_x(2)
+        load_x(3)
         nc.sync.dma_start(
             out=wk_raw[:].rearrange("p (g x) -> p g x", g=2),
             in_=Wk.rearrange("(g q t) c -> q g (t c)", g=2, q=P, t=4),
@@ -70,7 +74,7 @@ def tile_diffucoderattention_pa_t_kernel(tc, hidden_states, Wq, Wk, Wv, out_0, o
             out=wv_raw[:].rearrange("p (g x) -> p g x", g=2),
             in_=Wv.rearrange("(g q t) c -> q g (t c)", g=2, q=P, t=4),
         )
-        for ci in range(2, len(X_CHUNKS)):
+        for ci in range(4, len(X_CHUNKS)):
             load_x(ci)
 
         pos_i = const.tile([P, TPP], I32, name="pos_i")
@@ -150,8 +154,8 @@ def tile_diffucoderattention_pa_t_kernel(tc, hidden_states, Wq, Wk, Wv, out_0, o
             return xg
 
         def quantise_x(xg):
-            xc = work.tile([P, 512], U32, name="xc", tag="xc", align_bytes=64)
-            xs = work.tile([P, 512], U8, name="xs", tag="xs", align_bytes=64)
+            xc = work.tile([P, 512], U32, name="xc", tag="xc", align_bytes=64, bufs=6)
+            xs = work.tile([P, 512], U8, name="xs", tag="xs", align_bytes=64, bufs=6)
             nc.vector.quantize_mx(out=xc[:].bitcast(FP8X4), scales=xs[:], in_=xg[:])
             return xc, xs
 
@@ -179,37 +183,39 @@ def tile_diffucoderattention_pa_t_kernel(tc, hidden_states, Wq, Wk, Wv, out_0, o
                 in_=wg_v[:, g, c0:c1, :].rearrange("p c t -> p (c t)"),
             )
 
+        def tab_sin():
+            nc.vector.tensor_tensor(
+                out=tab[:, :, 1].rearrange("p q a (i e) -> p q (a i) e", e=2),
+                in0=sin_half[:].rearrange("p (q x) -> p q x", q=4).unsqueeze(3).to_broadcast([P, 4, 64, 2]),
+                in1=sign2[:].unsqueeze(1).unsqueeze(1).to_broadcast([P, 4, 64, 2]),
+                op=ALU.mult,
+            )
+
+        def tab_cos():
+            nc.vector.tensor_scalar(
+                out=tab[:, :, 0].rearrange("p q a (i e) -> p q (a i) e", e=2),
+                in0=sq_h[:].rearrange("p (q x) -> p q x", q=4).unsqueeze(3).to_broadcast([P, 4, 64, 2]),
+                scalar1=-2.0,
+                scalar2=1.0,
+                op0=ALU.mult,
+                op1=ALU.add,
+            )
+
+        xg_of[0] = evacuate(transposes(0))
         regroup_q(nc.vector.tensor_copy, 0, 0)
         regroup_q(nc.scalar.copy, 0, 1)
         nc.vector.tensor_tensor(out=sin_half[:], in0=sin_h[:], in1=cos_h[:], op=ALU.mult)
         regroup_q(nc.vector.tensor_copy, 1, 0)
         regroup_q(nc.scalar.copy, 1, 1)
-        xg_of[0] = evacuate(transposes(0))
-        xg_of[1] = evacuate(transposes(1))
+        xq_of[0] = quantise_x(xg_of[0])
         quantise_w(0, 0, 256)
         quantise_w(1, 0, 256)
+        tab_sin()
         quantise_w(0, 256, 512)
         quantise_w(1, 256, 512)
-        nc.vector.tensor_tensor(
-            out=tab[:, :, 1].rearrange("p q a (i e) -> p q (a i) e", e=2),
-            in0=sin_half[:].rearrange("p (q x) -> p q x", q=4).unsqueeze(3).to_broadcast([P, 4, 64, 2]),
-            in1=sign2[:].unsqueeze(1).unsqueeze(1).to_broadcast([P, 4, 64, 2]),
-            op=ALU.mult,
-        )
-        xq_of[0] = quantise_x(xg_of[0])
-        regroup_kv(wk_raw, 512)
+        tab_cos()
+        xg_of[1] = evacuate(transposes(1))
         xq_of[1] = quantise_x(xg_of[1])
-        regroup_kv(wv_raw, 640)
-        quantise_w(0, 512, 768)
-        quantise_w(1, 512, 768)
-        nc.vector.tensor_scalar(
-            out=tab[:, :, 0].rearrange("p q a (i e) -> p q (a i) e", e=2),
-            in0=sq_h[:].rearrange("p (q x) -> p q x", q=4).unsqueeze(3).to_broadcast([P, 4, 64, 2]),
-            scalar1=-2.0,
-            scalar2=1.0,
-            op0=ALU.mult,
-            op1=ALU.add,
-        )
 
         banks_of = {}
         q_tile_of = {}
@@ -230,16 +236,18 @@ def tile_diffucoderattention_pa_t_kernel(tc, hidden_states, Wq, Wk, Wv, out_0, o
                         stop=(g == 1),
                     )
 
-        def out_tiles(n):
+        def q_out_tile(n):
             for grp in Q_GROUPS:
                 if grp[0] == n:
                     qo = outp.tile([P, len(grp) * 8, P], F32, name="qo", tag="qo")
                     for k, m in enumerate(grp):
                         q_tile_of[m] = (qo, k, grp)
+
+        def kv_out_tiles(n):
             for grp in KV_GROUPS:
                 if grp[0] == n:
-                    ko = outp.tile([P, len(grp) * 2, P], F32, name="ko", tag="ko", bufs=3)
-                    vo = outp.tile([P, len(grp) * 2, P], F32, name="vo", tag="vo", bufs=3)
+                    ko = outp.tile([P, len(grp) * 2, P], F32, name="ko", tag="ko", bufs=6)
+                    vo = outp.tile([P, len(grp) * 2, P], F32, name="vo", tag="vo", bufs=4)
                     for k, m in enumerate(grp):
                         kv_tile_of[m] = (ko, vo, k, grp)
 
@@ -289,16 +297,11 @@ def tile_diffucoderattention_pa_t_kernel(tc, hidden_states, Wq, Wk, Wv, out_0, o
                 op=ALU.mult,
             )
             rope_tmp[("k", n)] = t12
-            ko, vo, k, grp = kv_tile_of[n]
-            nc.vector.tensor_copy(
-                out=ko[:, 2 * k : 2 * k + 2, 64:128],
-                in_=banks_of[n][2][:].rearrange("p (a s f) -> p a s f", a=2, s=4)[:, :, 1, :],
-            )
 
-        def rope_k_add(n):
+        def rope_k_add(n, eng):
             ko, vo, k, grp = kv_tile_of[n]
             t12 = rope_tmp[("k", n)]
-            nc.vector.tensor_tensor(
+            eng.tensor_tensor(
                 out=ko[:, 2 * k : 2 * k + 2, 0:64].rearrange("p a (i e) -> p a i e", e=2),
                 in0=t12[:, 0].rearrange("p a (i e) -> p a i e", e=2),
                 in1=t12[:, 1].rearrange("p a (i e) -> p a i e", e=2)[:, :, :, ::-1],
@@ -317,6 +320,10 @@ def tile_diffucoderattention_pa_t_kernel(tc, hidden_states, Wq, Wk, Wv, out_0, o
             nc.scalar.copy(
                 out=vo[:, 2 * k : 2 * k + 2, :], in_=bank_k[:].rearrange("p (a s f) -> p a s f", a=2, s=2)[:, :, 1, :]
             )
+            nc.scalar.copy(
+                out=ko[:, 2 * k : 2 * k + 2, 64:128],
+                in_=bank_k[:].rearrange("p (a s f) -> p a s f", a=2, s=4)[:, :, 1, :],
+            )
 
         def store_q(n):
             qo, k, grp = q_tile_of[n]
@@ -328,75 +335,73 @@ def tile_diffucoderattention_pa_t_kernel(tc, hidden_states, Wq, Wk, Wv, out_0, o
                 out=dst[:, j0 * 512 : (j0 + 2 * len(grp)) * 512], in_=qo[:].rearrange("p m d -> p (m d)")
             )
 
-        def store_kv(n):
-            ko, vo, k, grp = kv_tile_of[n]
+        def store_kv(n, which):
+            grp = kv_tile_of[n][3]
             if grp[-1] != n:
                 return
             b, j0 = grp[0] // 4, 2 * (grp[0] % 4)
-            for dram, sb in ((out_1, ko), (out_2, vo)):
-                dst = dram[b].rearrange("(p j) o d -> p (j o d)", j=TPP)
-                nc.sync.dma_start(
-                    out=dst[:, j0 * P : (j0 + 2 * len(grp)) * P], in_=sb[:].rearrange("p m d -> p (m d)")
-                )
-
-        def new_banks(n):
-            out_tiles(n)
-            bank_r = psum.tile([P, 512], F32, name="bank_r", tag="bank_r")
-            bank_p = psum.tile([P, 512], F32, name="bank_p", tag="bank_p")
-            bank_k = psum.tile([P, 512], F32, name="bank_k", tag="bank_k")
-            banks_of[n] = (bank_r, bank_p, bank_k)
-
-        def mx_q(n):
-            mx(n, banks_of[n][0], 0)
-            mx(n, banks_of[n][1], 256)
-            copy_q(n)
-
-        def mx_kv(n):
-            mx(n, banks_of[n][2], 512)
-            copy_kv(n)
+            dst = (out_1, out_2)[which][b].rearrange("(p j) o d -> p (j o d)", j=TPP)
+            nc.sync.dma_start(
+                out=dst[:, j0 * P : (j0 + 2 * len(grp)) * P],
+                in_=kv_tile_of[n][which][:].rearrange("p m d -> p (m d)"),
+            )
 
         def ahead(n):
             if n < NPAIR:
                 xg_of[n] = evacuate(transposes(n))
 
-        def vector_part(n):
-            rope_q_mul(n)
-            rope_q_add(n, nc.gpsimd)
-            store_q(n)
-            if n + 2 < NPAIR:
-                xq_of[n + 2] = quantise_x(xg_of[n + 2])
-            if n > 0:
-                rope_k_add(n - 1)
-                store_kv(n - 1)
-            rope_k_mul(n)
-
-        new_banks(0)
-        new_banks(1)
-        mx_q(0)
-        mx_q(1)
-        ahead(2)
-        mx_kv(0)
-        mx_kv(1)
-        ahead(3)
-        vector_part(0)
-        vector_part(1)
-        for n in range(2, NPAIR - 1):
-            new_banks(n)
-            mx_q(n)
-            ahead(n + 2)
-            mx_kv(n)
-            vector_part(n)
+        def kv_passes(j):
+            kv_out_tiles(j)
+            bank_k = psum.tile([P, 512], F32, name="bank_k", tag="bank_k")
+            banks_of[j] = banks_of[j][:2] + (bank_k,)
+            mx(j, bank_k, 512)
+            copy_kv(j)
+            store_kv(j, 1)
 
         last = NPAIR - 1
-        new_banks(last)
-        mx_kv(last)
-        mx_q(last)
-        rope_k_add(last - 1)
-        store_kv(last - 1)
+        for n in range(NPAIR):
+            j = n - K_LAG
+            q_out_tile(n)
+            bank_r = psum.tile([P, 512], F32, name="bank_r", tag="bank_r")
+            bank_p = psum.tile([P, 512], F32, name="bank_p", tag="bank_p")
+            banks_of[n] = (bank_r, bank_p)
+            if j >= 1:
+                rope_k_add(j - 1, nc.gpsimd)
+                store_kv(j - 1, 0)
+            mx(n, bank_r, 0)
+            rope_q_mul(n)
+            if n < last:
+                rope_q_add(n, nc.gpsimd)
+            else:
+                rope_q_add(n, nc.gpsimd, 0, 4)
+            mx(n, bank_p, 256)
+            copy_q(n)
+            if n < last:
+                store_q(n)
+            if n == 0:
+                ahead(2)
+            ahead(n + T_AHEAD)
+            if n + 2 < NPAIR:
+                xq_of[n + 2] = quantise_x(xg_of[n + 2])
+            if n == 0:
+                regroup_kv(wk_raw, 512)
+            if n == 1:
+                regroup_kv(wv_raw, 640)
+                quantise_w(0, 512, 768)
+                quantise_w(1, 512, 768)
+            if j >= 0:
+                kv_passes(j)
+                rope_k_mul(j)
+        rope_q_add(last, nc.vector, 4, 8)
+        store_q_tile(last, 0)
+        store_q_tile(last, 1)
+        rope_k_add(last - K_LAG, nc.gpsimd)
+        store_kv(last - K_LAG, 0)
+        kv_passes(last - 1)
+        kv_passes(last)
+        rope_k_mul(last - 1)
+        rope_k_add(last - 1, nc.gpsimd)
+        store_kv(last - 1, 0)
         rope_k_mul(last)
-        rope_k_add(last)
-        store_kv(last)
-        rope_q_mul(last)
-        for a in range(2):
-            rope_q_add(last, nc.vector, 4 * a, 4 * a + 4)
-            store_q_tile(last, a)
+        rope_k_add(last, nc.vector)
+        store_kv(last, 0)

@@ -26,7 +26,7 @@ C1 = 51472.0 / 8192.0
 C2 = TWO_PI - C1
 
 X_CHUNKS = [(0, 0, 2), (0, 2, 2), (0, 4, 2), (0, 6, 2), (1, 0, 4), (1, 4, 4), (2, 0, 4), (2, 4, 4), (3, 0, 4), (3, 4, 4)]
-K_LAG = 2
+K_LAG = 3
 T_AHEAD = 3
 Q_GROUPS = [[0, 1], [2, 3], [4, 5], [6, 7], [8, 9], [10], [11], [12], [13], [14], [15]]
 KV_GROUPS = [[0, 1], [2, 3], [4, 5], [6, 7], [8, 9], [10, 11], [12], [13], [14], [15]]
@@ -130,9 +130,6 @@ def tile_diffucoderattention_pa_t_kernel(tc, hidden_states, Wq, Wk, Wv, out_0, o
         nc.vector.tensor_scalar(
             out=carg[:], in0=nabs[:], scalar1=0.5, scalar2=0.5 * math.pi, op0=ALU.mult, op1=ALU.add
         )
-        nc.scalar.activation(out=sin_h[:], in_=red[:], func=ACT.Sin, scale=0.5)
-        nc.scalar.activation(out=cos_h[:], in_=carg[:], func=ACT.Sin)
-        nc.scalar.activation(out=sq_h[:], in_=sin_h[:], func=ACT.Square)
 
         def transposes(n):
             xt, off = x_of_pair[n]
@@ -154,8 +151,8 @@ def tile_diffucoderattention_pa_t_kernel(tc, hidden_states, Wq, Wk, Wv, out_0, o
             return xg
 
         def quantise_x(xg):
-            xc = work.tile([P, 512], U32, name="xc", tag="xc", align_bytes=64, bufs=6)
-            xs = work.tile([P, 512], U8, name="xs", tag="xs", align_bytes=64, bufs=6)
+            xc = work.tile([P, 512], U32, name="xc", tag="xc", align_bytes=64, bufs=7)
+            xs = work.tile([P, 512], U8, name="xs", tag="xs", align_bytes=64, bufs=7)
             nc.vector.quantize_mx(out=xc[:].bitcast(FP8X4), scales=xs[:], in_=xg[:])
             return xc, xs
 
@@ -172,7 +169,7 @@ def tile_diffucoderattention_pa_t_kernel(tc, hidden_states, Wq, Wk, Wv, out_0, o
             copy(out=wg_v[:, g, s * 256 : (s + 1) * 256, :].rearrange("p (h f) t -> p h f t", h=4), in_=src[:, s])
 
         def regroup_kv(raw, c0):
-            nc.vector.tensor_copy(
+            nc.scalar.copy(
                 out=wg_v[:, :, c0 : c0 + P, :], in_=raw[:].rearrange("p (g t c) -> p g c t", g=2, t=4, c=P)
             )
 
@@ -202,20 +199,24 @@ def tile_diffucoderattention_pa_t_kernel(tc, hidden_states, Wq, Wk, Wv, out_0, o
             )
 
         xg_of[0] = evacuate(transposes(0))
+        nc.scalar.activation(out=sin_h[:], in_=red[:], func=ACT.Sin, scale=0.5)
+        nc.scalar.activation(out=cos_h[:], in_=carg[:], func=ACT.Sin)
+        nc.scalar.activation(out=sq_h[:], in_=sin_h[:], func=ACT.Square)
         regroup_q(nc.vector.tensor_copy, 0, 0)
         regroup_q(nc.scalar.copy, 0, 1)
-        nc.vector.tensor_tensor(out=sin_half[:], in0=sin_h[:], in1=cos_h[:], op=ALU.mult)
-        regroup_q(nc.vector.tensor_copy, 1, 0)
-        regroup_q(nc.scalar.copy, 1, 1)
         xq_of[0] = quantise_x(xg_of[0])
+        regroup_q(nc.vector.tensor_copy, 1, 0)
         quantise_w(0, 0, 256)
         quantise_w(1, 0, 256)
-        tab_sin()
+        regroup_q(nc.vector.tensor_copy, 1, 1)
         quantise_w(0, 256, 512)
         quantise_w(1, 256, 512)
-        tab_cos()
         xg_of[1] = evacuate(transposes(1))
+        xg_of[2] = evacuate(transposes(2))
         xq_of[1] = quantise_x(xg_of[1])
+        nc.vector.tensor_tensor(out=sin_half[:], in0=sin_h[:], in1=cos_h[:], op=ALU.mult)
+        tab_sin()
+        tab_cos()
 
         banks_of = {}
         q_tile_of = {}
@@ -378,8 +379,6 @@ def tile_diffucoderattention_pa_t_kernel(tc, hidden_states, Wq, Wk, Wv, out_0, o
             copy_q(n)
             if n < last:
                 store_q(n)
-            if n == 0:
-                ahead(2)
             ahead(n + T_AHEAD)
             if n + 2 < NPAIR:
                 xq_of[n + 2] = quantise_x(xg_of[n + 2])
@@ -387,6 +386,7 @@ def tile_diffucoderattention_pa_t_kernel(tc, hidden_states, Wq, Wk, Wv, out_0, o
                 regroup_kv(wk_raw, 512)
             if n == 1:
                 regroup_kv(wv_raw, 640)
+            if n == 2:
                 quantise_w(0, 512, 768)
                 quantise_w(1, 512, 768)
             if j >= 0:
@@ -395,13 +395,10 @@ def tile_diffucoderattention_pa_t_kernel(tc, hidden_states, Wq, Wk, Wv, out_0, o
         rope_q_add(last, nc.vector, 4, 8)
         store_q_tile(last, 0)
         store_q_tile(last, 1)
-        rope_k_add(last - K_LAG, nc.gpsimd)
-        store_kv(last - K_LAG, 0)
-        kv_passes(last - 1)
-        kv_passes(last)
-        rope_k_mul(last - 1)
-        rope_k_add(last - 1, nc.gpsimd)
-        store_kv(last - 1, 0)
-        rope_k_mul(last)
+        for j in range(NPAIR - K_LAG, NPAIR):
+            rope_k_add(j - 1, nc.gpsimd)
+            store_kv(j - 1, 0)
+            kv_passes(j)
+            rope_k_mul(j)
         rope_k_add(last, nc.vector)
         store_kv(last, 0)

@@ -29,7 +29,7 @@ X_CHUNKS = [(0, 0, 2), (0, 2, 2), (0, 4, 2), (0, 6, 2), (1, 0, 4), (1, 4, 4), (2
 K_LAG = 3
 T_AHEAD = 3
 Q_GROUPS = [[0, 1], [2, 3], [4, 5], [6, 7], [8, 9], [10], [11], [12], [13], [14], [15]]
-KV_GROUPS = [[0, 1], [2, 3], [4, 5], [6, 7], [8, 9], [10, 11], [12], [13], [14], [15]]
+KV_GROUPS = [[0, 1], [2, 3], [4, 5], [6, 7], [8, 9], [10, 11], [12, 13], [14, 15]]
 
 
 def tile_diffucoderattention_pa_t_kernel(tc, hidden_states, Wq, Wk, Wv, out_0, out_1, out_2):
@@ -248,7 +248,7 @@ def tile_diffucoderattention_pa_t_kernel(tc, hidden_states, Wq, Wk, Wv, out_0, o
             for grp in KV_GROUPS:
                 if grp[0] == n:
                     ko = outp.tile([P, len(grp) * 2, P], F32, name="ko", tag="ko", bufs=6)
-                    vo = outp.tile([P, len(grp) * 2, P], F32, name="vo", tag="vo", bufs=4)
+                    vo = outp.tile([P, len(grp) * 2, P], F32, name="vo", tag="vo", bufs=6)
                     for k, m in enumerate(grp):
                         kv_tile_of[m] = (ko, vo, k, grp)
 
@@ -351,9 +351,9 @@ def tile_diffucoderattention_pa_t_kernel(tc, hidden_states, Wq, Wk, Wv, out_0, o
             if n < NPAIR:
                 xg_of[n] = evacuate(transposes(n))
 
-        def kv_passes(j):
+        def kv_passes(j, tag="bank_k"):
             kv_out_tiles(j)
-            bank_k = psum.tile([P, 512], F32, name="bank_k", tag="bank_k")
+            bank_k = psum.tile([P, 512], F32, name="bank_k", tag=tag, bufs=(2 if tag == "bank_k" else 1))
             banks_of[j] = banks_of[j][:2] + (bank_k,)
             mx(j, bank_k, 512)
             copy_kv(j)
@@ -373,8 +373,6 @@ def tile_diffucoderattention_pa_t_kernel(tc, hidden_states, Wq, Wk, Wv, out_0, o
             rope_q_mul(n)
             if n < last:
                 rope_q_add(n, nc.gpsimd)
-            else:
-                rope_q_add(n, nc.gpsimd, 0, 4)
             mx(n, bank_p, 256)
             copy_q(n)
             if n < last:
@@ -392,13 +390,17 @@ def tile_diffucoderattention_pa_t_kernel(tc, hidden_states, Wq, Wk, Wv, out_0, o
             if j >= 0:
                 kv_passes(j)
                 rope_k_mul(j)
-        rope_q_add(last, nc.vector, 4, 8)
-        store_q_tile(last, 0)
-        store_q_tile(last, 1)
-        for j in range(NPAIR - K_LAG, NPAIR):
-            rope_k_add(j - 1, nc.gpsimd)
-            store_kv(j - 1, 0)
-            kv_passes(j)
-            rope_k_mul(j)
+        kv_passes(last - 2)
+        rope_k_mul(last - 2)
+        rope_q_add(last, nc.vector)
+        store_q(last)
+        rope_k_add(last - 3, nc.gpsimd)
+        rope_k_add(last - 2, nc.gpsimd)
+        store_kv(last - 2, 0)
+        kv_passes(last - 1, "tp0")
+        rope_k_mul(last - 1)
+        kv_passes(last, "tp1")
+        rope_k_mul(last)
+        rope_k_add(last - 1, nc.vector)
         rope_k_add(last, nc.vector)
         store_kv(last, 0)

@@ -375,8 +375,6 @@ def tile_diffucoderattention_pa_t_kernel(tc, hidden_states, Wq, Wk, Wv, out_0, o
                 rope_q_add(n, nc.gpsimd)
             mx(n, bank_p, 256)
             copy_q(n)
-            if n < last:
-                store_q(n)
             ahead(n + T_AHEAD)
             if n + 2 < NPAIR:
                 xq_of[n + 2] = quantise_x(xg_of[n + 2])
@@ -390,6 +388,8 @@ def tile_diffucoderattention_pa_t_kernel(tc, hidden_states, Wq, Wk, Wv, out_0, o
             if j >= 0:
                 kv_passes(j)
                 rope_k_mul(j)
+            if n < last:
+                store_q(n)
         kv_passes(last - 2)
         rope_k_mul(last - 2)
         rope_q_add(last, nc.vector)

@@ -27,6 +27,7 @@ C2 = TWO_PI - C1
 
 X_CHUNKS = [(0, 0, 2), (0, 2, 2), (0, 4, 2), (0, 6, 2), (1, 0, 4), (1, 4, 4), (2, 0, 4), (2, 4, 4), (3, 0, 4), (3, 4, 4)]
 K_LAG = 3
+FINE_FROM = 13
 T_AHEAD = 3
 Q_GROUPS = [[0, 1], [2, 3], [4, 5], [6, 7], [8, 9], [10], [11], [12], [13], [14], [15]]
 KV_GROUPS = [[0, 1], [2, 3], [4, 5], [6, 7], [8, 9], [10, 11], [12, 13], [14, 15]]
@@ -212,7 +213,6 @@ def tile_diffucoderattention_pa_t_kernel(tc, hidden_states, Wq, Wk, Wv, out_0, o
         quantise_w(0, 256, 512)
         quantise_w(1, 256, 512)
         xg_of[1] = evacuate(transposes(1))
-        xg_of[2] = evacuate(transposes(2))
         xq_of[1] = quantise_x(xg_of[1])
         nc.vector.tensor_tensor(out=sin_half[:], in0=sin_h[:], in1=cos_h[:], op=ALU.mult)
         tab_sin()
@@ -371,8 +371,13 @@ def tile_diffucoderattention_pa_t_kernel(tc, hidden_states, Wq, Wk, Wv, out_0, o
                 store_kv(j - 1, 0)
             mx(n, bank_r, 0)
             rope_q_mul(n)
-            if n < last:
+            if n < FINE_FROM:
                 rope_q_add(n, nc.gpsimd)
+            elif n < last:
+                rope_q_add(n, nc.gpsimd, 0, 4)
+                rope_q_add(n, nc.gpsimd, 4, 8)
+            if n == 0:
+                ahead(2)
             mx(n, bank_p, 256)
             copy_q(n)
             ahead(n + T_AHEAD)
@@ -388,8 +393,11 @@ def tile_diffucoderattention_pa_t_kernel(tc, hidden_states, Wq, Wk, Wv, out_0, o
             if j >= 0:
                 kv_passes(j)
                 rope_k_mul(j)
-            if n < last:
+            if n < FINE_FROM:
                 store_q(n)
+            elif n < last:
+                store_q_tile(n, 0)
+                store_q_tile(n, 1)
         kv_passes(last - 2)
         rope_k_mul(last - 2)
         rope_q_add(last, nc.vector)

@@ -166,12 +166,16 @@ def tile_diffucoderattention_pa_t_kernel(tc, hidden_states, Wq, Wk, Wv, out_0, o
         ws = const.tile([P, 2, 768], U8, name="ws", align_bytes=64)
 
         def regroup_q(copy, g, s):
-            src = wq_raw[g][:].rearrange("p (t h s f) -> p s h f t", t=4, h=4, s=2, f=64)
-            copy(out=wg_v[:, g, s * 256 : (s + 1) * 256, :].rearrange("p (h f) t -> p h f t", h=4), in_=src[:, s])
+            src = wq_raw[g][:].rearrange("p (t h s c i) -> p s h c t i", t=4, h=4, s=2, c=16, i=4)
+            copy(
+                out=wg_v[:, g, s * 256 : (s + 1) * 256, :].rearrange("p (h c i) t -> p h c t i", h=4, i=4),
+                in_=src[:, s],
+            )
 
         def regroup_kv(raw, c0):
             nc.scalar.copy(
-                out=wg_v[:, :, c0 : c0 + P, :], in_=raw[:].rearrange("p (g t c) -> p g c t", g=2, t=4, c=P)
+                out=wg_v[:, :, c0 : c0 + P, :].rearrange("p g (c i) t -> p g c t i", i=4),
+                in_=raw[:].rearrange("p (g t c i) -> p g c t i", g=2, t=4, i=4),
             )
 
         def quantise_w(g, c0, c1):

@@ -262,11 +262,11 @@ def tile_diffucoderattention_pa_t_kernel(tc, hidden_states, Wq, Wk, Wv, out_0, o
             t12 = rope.tile([P, 2, 512], F32, name="t12q", tag="t12q")
             nc.vector.tensor_tensor(
                 out=t12[:].rearrange("p c (a h f) -> p c a h f", a=2, h=4),
-                in0=banks_of[n][0][:]
+                in0=tab[:, n % 4].unsqueeze(3).to_broadcast([P, 2, 2, 4, 64]),
+                in1=banks_of[n][0][:]
                 .rearrange("p (a h f) -> p a h f", a=2, h=4)
                 .unsqueeze(1)
                 .to_broadcast([P, 2, 2, 4, 64]),
-                in1=tab[:, n % 4].unsqueeze(3).to_broadcast([P, 2, 2, 4, 64]),
                 op=ALU.mult,
             )
             rope_tmp[("q", n)] = t12
@@ -294,11 +294,11 @@ def tile_diffucoderattention_pa_t_kernel(tc, hidden_states, Wq, Wk, Wv, out_0, o
             t12 = rope.tile([P, 2, 2, 64], F32, name="t12k", tag="t12k")
             nc.vector.tensor_tensor(
                 out=t12[:],
-                in0=banks_of[n][2][:]
+                in0=tab[:, n % 4],
+                in1=banks_of[n][2][:]
                 .rearrange("p (a s f) -> p a s f", a=2, s=4)[:, :, 0, :]
                 .unsqueeze(1)
                 .to_broadcast([P, 2, 2, 64]),
-                in1=tab[:, n % 4],
                 op=ALU.mult,
             )
             rope_tmp[("k", n)] = t12

@@ -29,6 +29,8 @@ X_CHUNKS = [(0, 0, 2), (0, 2, 2), (0, 4, 2), (0, 6, 2), (1, 0, 4), (1, 4, 4), (2
 K_LAG = 3
 FINE_FROM = 13
 T_AHEAD = 3
+SORT_FROM = 7
+KV_VECTOR_TO = 9
 Q_GROUPS = [[0, 1], [2, 3], [4, 5], [6, 7], [8, 9], [10], [11], [12], [13], [14], [15]]
 KV_GROUPS = [[0, 1], [2, 3], [4, 5], [6, 7], [8, 9], [10, 11], [12, 13], [14, 15]]
 
@@ -138,11 +140,27 @@ def tile_diffucoderattention_pa_t_kernel(tc, hidden_states, Wq, Wk, Wv, out_0, o
             banks = []
             for a in range(2):
                 tp = psum.tile([P, 4, P], F32, name="tp%d" % a, tag="tp%d" % a, bufs=1)
+                if a == 0 and n in sorted_of:
+                    for v in range(4):
+                        nc.tensor.transpose(tp[:, v, :], sorted_of[n][:, v, :], ident[:])
+                    banks.append(tp)
+                    continue
                 for v in range(4):
                     c0 = (off + a) * 512 + (v // 2) * 256 + v % 2
                     nc.tensor.transpose(tp[:, v, :], xw[:, c0 : c0 + 255 : 2], ident[:])
                 banks.append(tp)
             return banks
+
+        sorted_of = {}
+
+        def sort_words(n):
+            xt, off = x_of_pair[n]
+            so = work.tile([P, 4, P], F32, name="so", tag="so", bufs=3)
+            nc.scalar.copy(
+                out=so[:].rearrange("p (g u) r -> p g u r", u=2),
+                in_=xt[:, off * E : (off + 1) * E].bitcast(F32).rearrange("p (g r u) -> p g u r", g=2, u=2),
+            )
+            sorted_of[n] = so
 
         def evacuate(banks):
             xg = work.tile([P, 2048], BF16, name="xg", tag="xg", align_bytes=64)
@@ -322,10 +340,11 @@ def tile_diffucoderattention_pa_t_kernel(tc, hidden_states, Wq, Wk, Wv, out_0, o
         def copy_kv(n):
             bank_k = banks_of[n][2]
             ko, vo, k, grp = kv_tile_of[n]
-            nc.scalar.copy(
+            copy = nc.vector.tensor_copy if n <= KV_VECTOR_TO else nc.scalar.copy
+            copy(
                 out=vo[:, 2 * k : 2 * k + 2, :], in_=bank_k[:].rearrange("p (a s f) -> p a s f", a=2, s=2)[:, :, 1, :]
             )
-            nc.scalar.copy(
+            copy(
                 out=ko[:, 2 * k : 2 * k + 2, 64:128],
                 in_=bank_k[:].rearrange("p (a s f) -> p a s f", a=2, s=4)[:, :, 1, :],
             )
@@ -384,6 +403,8 @@ def tile_diffucoderattention_pa_t_kernel(tc, hidden_states, Wq, Wk, Wv, out_0, o
                 ahead(2)
             mx(n, bank_p, 256)
             copy_q(n)
+            if SORT_FROM <= n + T_AHEAD + 1 < NPAIR:
+                sort_words(n + T_AHEAD + 1)
             ahead(n + T_AHEAD)
             if n + 2 < NPAIR:
                 xq_of[n + 2] = quantise_x(xg_of[n + 2])

@@ -109,8 +109,8 @@ def tile_diffucoderattention_pa_t_kernel(tc, hidden_states, Wq, Wk, Wv, out_0, o
 
         nc.vector.tensor_copy(out=pos_f[:], in_=pos_i[:])
         nc.vector.memset(freq[:, 0:1], 1.0)
-        nc.vector.memset(sign2[:, 0:1], 2.0)
-        nc.vector.memset(sign2[:, 1:2], -2.0)
+        nc.vector.memset(sign2[:, 0:1], -2.0)
+        nc.vector.memset(sign2[:, 1:2], 2.0)
         w = 1
         while w < 32:
             nc.vector.tensor_scalar(
@@ -278,13 +278,17 @@ def tile_diffucoderattention_pa_t_kernel(tc, hidden_states, Wq, Wk, Wv, out_0, o
 
         def rope_q_mul(n):
             t12 = rope.tile([P, 2, 512], F32, name="t12q", tag="t12q")
+            bank = banks_of[n][0][:]
             nc.vector.tensor_tensor(
-                out=t12[:].rearrange("p c (a h f) -> p c a h f", a=2, h=4),
-                in0=tab[:, n % 4].unsqueeze(3).to_broadcast([P, 2, 2, 4, 64]),
-                in1=banks_of[n][0][:]
-                .rearrange("p (a h f) -> p a h f", a=2, h=4)
-                .unsqueeze(1)
-                .to_broadcast([P, 2, 2, 4, 64]),
+                out=t12[:, 0].rearrange("p (a h f) -> p a h f", a=2, h=4),
+                in0=tab[:, n % 4, 0].unsqueeze(2).to_broadcast([P, 2, 4, 64]),
+                in1=bank.rearrange("p (a h f) -> p a h f", a=2, h=4),
+                op=ALU.mult,
+            )
+            nc.vector.tensor_tensor(
+                out=t12[:, 1].rearrange("p (a h i e) -> p a h i e", a=2, h=4, e=2),
+                in0=tab[:, n % 4, 1].rearrange("p a (i e) -> p a i e", e=2).unsqueeze(2).to_broadcast([P, 2, 4, 32, 2]),
+                in1=bank.rearrange("p (a h i e) -> p a h i e", a=2, h=4, e=2)[:, :, :, :, ::-1],
                 op=ALU.mult,
             )
             rope_tmp[("q", n)] = t12
@@ -293,9 +297,9 @@ def tile_diffucoderattention_pa_t_kernel(tc, hidden_states, Wq, Wk, Wv, out_0, o
             qo, k, grp = q_tile_of[n]
             t12 = rope_tmp[("q", n)]
             eng.tensor_tensor(
-                out=qo[:, 8 * k + m0 : 8 * k + m1, 0:64].rearrange("p m (i e) -> p m i e", e=2),
-                in0=t12[:, 0].rearrange("p (m i e) -> p m i e", m=8, e=2)[:, m0:m1],
-                in1=t12[:, 1].rearrange("p (m i e) -> p m i e", m=8, e=2)[:, m0:m1, :, ::-1],
+                out=qo[:, 8 * k + m0 : 8 * k + m1, 0:64],
+                in0=t12[:, 0].rearrange("p (m f) -> p m f", m=8)[:, m0:m1],
+                in1=t12[:, 1].rearrange("p (m f) -> p m f", m=8)[:, m0:m1],
                 op=ALU.add,
             )
 
@@ -310,13 +314,17 @@ def tile_diffucoderattention_pa_t_kernel(tc, hidden_states, Wq, Wk, Wv, out_0, o
 
         def rope_k_mul(n):
             t12 = rope.tile([P, 2, 2, 64], F32, name="t12k", tag="t12k")
+            bank = banks_of[n][2][:]
             nc.vector.tensor_tensor(
-                out=t12[:],
-                in0=tab[:, n % 4],
-                in1=banks_of[n][2][:]
-                .rearrange("p (a s f) -> p a s f", a=2, s=4)[:, :, 0, :]
-                .unsqueeze(1)
-                .to_broadcast([P, 2, 2, 64]),
+                out=t12[:, 0],
+                in0=tab[:, n % 4, 0],
+                in1=bank.rearrange("p (a s f) -> p a s f", a=2, s=4)[:, :, 0, :],
+                op=ALU.mult,
+            )
+            nc.vector.tensor_tensor(
+                out=t12[:, 1].rearrange("p a (i e) -> p a i e", e=2),
+                in0=tab[:, n % 4, 1].rearrange("p a (i e) -> p a i e", e=2),
+                in1=bank.rearrange("p (a s i e) -> p a s i e", a=2, s=4, e=2)[:, :, 0, :, ::-1],
                 op=ALU.mult,
             )
             rope_tmp[("k", n)] = t12
@@ -325,9 +333,9 @@ def tile_diffucoderattention_pa_t_kernel(tc, hidden_states, Wq, Wk, Wv, out_0, o
             ko, vo, k, grp = kv_tile_of[n]
             t12 = rope_tmp[("k", n)]
             eng.tensor_tensor(
-                out=ko[:, 2 * k : 2 * k + 2, 0:64].rearrange("p a (i e) -> p a i e", e=2),
-                in0=t12[:, 0].rearrange("p a (i e) -> p a i e", e=2),
-                in1=t12[:, 1].rearrange("p a (i e) -> p a i e", e=2)[:, :, :, ::-1],
+                out=ko[:, 2 * k : 2 * k + 2, 0:64],
+                in0=t12[:, 0],
+                in1=t12[:, 1],
                 op=ALU.add,
             )
 

@@ -32,6 +32,7 @@ T_AHEAD = 3
 SORT_FROM = 7
 KV_VECTOR_TO = 9
 Q_GROUPS = [[0, 1], [2, 3], [4, 5], [6, 7], [8, 9], [10], [11], [12], [13], [14], [15]]
+K_SHIFT = 4
 KV_GROUPS = [[0, 1], [2, 3], [4, 5], [6, 7], [8, 9], [10, 11], [12, 13], [14, 15]]
 
 
@@ -259,17 +260,24 @@ def tile_diffucoderattention_pa_t_kernel(tc, hidden_states, Wq, Wk, Wv, out_0, o
                         stop=(g == 1),
                     )
 
+        def q_rows(n):
+            qo, i, grp, t12 = q_tile_of[n]
+            return (10 * i, 2, 0) if i == 0 else (10 * i, 0, 8)
+
         def q_out_tile(n):
             for grp in Q_GROUPS:
                 if grp[0] == n:
-                    qo = outp.tile([P, len(grp) * 8, P], F32, name="qo", tag="qo")
-                    for k, m in enumerate(grp):
-                        q_tile_of[m] = (qo, k, grp)
+                    qo = outp.tile([P, len(grp) * 10, P], F32, name="qo", tag="qo")
+                    for i, m in enumerate(grp):
+                        q_tile_of[m] = [qo, i, grp, None]
+            q_tile_of[n][3] = rope.tile([P, 2, 10, 64], F32, name="t12q", tag="t12q")
 
         def kv_out_tiles(n):
             for grp in KV_GROUPS:
                 if grp[0] == n:
-                    ko = outp.tile([P, len(grp) * 2, P], F32, name="ko", tag="ko", bufs=6)
+                    ko = None
+                    if n + K_SHIFT >= NPAIR:
+                        ko = outp.tile([P, len(grp) * 2, P], F32, name="ko", tag="ko", bufs=2)
                     vo = outp.tile([P, len(grp) * 2, P], F32, name="vo", tag="vo", bufs=6)
                     for k, m in enumerate(grp):
                         kv_tile_of[m] = (ko, vo, k, grp)
@@ -277,43 +285,47 @@ def tile_diffucoderattention_pa_t_kernel(tc, hidden_states, Wq, Wk, Wv, out_0, o
         rope_tmp = {}
 
         def rope_q_mul(n):
-            t12 = rope.tile([P, 2, 512], F32, name="t12q", tag="t12q")
+            r0, rq, rk = q_rows(n)
+            t12 = q_tile_of[n][3][:, :, rq : rq + 8, :].rearrange("p c (a h) f -> p c a h f", a=2)
             bank = banks_of[n][0][:]
             nc.vector.tensor_tensor(
-                out=t12[:, 0].rearrange("p (a h f) -> p a h f", a=2, h=4),
+                out=t12[:, 0],
                 in0=tab[:, n % 4, 0].unsqueeze(2).to_broadcast([P, 2, 4, 64]),
                 in1=bank.rearrange("p (a h f) -> p a h f", a=2, h=4),
                 op=ALU.mult,
             )
             nc.vector.tensor_tensor(
-                out=t12[:, 1].rearrange("p (a h i e) -> p a h i e", a=2, h=4, e=2),
+                out=t12[:, 1].rearrange("p a h (i e) -> p a h i e", e=2),
                 in0=tab[:, n % 4, 1].rearrange("p a (i e) -> p a i e", e=2).unsqueeze(2).to_broadcast([P, 2, 4, 32, 2]),
                 in1=bank.rearrange("p (a h i e) -> p a h i e", a=2, h=4, e=2)[:, :, :, :, ::-1],
                 op=ALU.mult,
             )
-            rope_tmp[("q", n)] = t12
 
-        def rope_q_add(n, eng, m0=0, m1=8):
-            qo, k, grp = q_tile_of[n]
-            t12 = rope_tmp[("q", n)]
+        def rope_q_add(n, eng, m0=0, m1=10):
+            qo, i, grp, t12 = q_tile_of[n]
+            if n < K_SHIFT:
+                m0 = q_rows(n)[1]
+                m1 = m0 + 8
             eng.tensor_tensor(
-                out=qo[:, 8 * k + m0 : 8 * k + m1, 0:64],
-                in0=t12[:, 0].rearrange("p (m f) -> p m f", m=8)[:, m0:m1],
-                in1=t12[:, 1].rearrange("p (m f) -> p m f", m=8)[:, m0:m1],
-                op=ALU.add,
+                out=qo[:, 10 * i + m0 : 10 * i + m1, 0:64], in0=t12[:, 0, m0:m1], in1=t12[:, 1, m0:m1], op=ALU.add
             )
 
         def store_q_tile(n, a):
-            qo, k, grp = q_tile_of[n]
+            qo = q_tile_of[n][0]
             b, j = n // 4, 2 * (n % 4) + a
             dst = out_0[b].rearrange("(p j) h d -> p (j h d)", j=TPP)
             nc.sync.dma_start(
                 out=dst[:, j * 512 : (j + 1) * 512],
-                in_=qo[:, 8 * k + 4 * a : 8 * k + 4 * a + 4, :].rearrange("p m d -> p (m d)"),
+                in_=qo[:, 2 + 4 * a : 6 + 4 * a, :].rearrange("p m d -> p (m d)"),
             )
 
         def rope_k_mul(n):
-            t12 = rope.tile([P, 2, 2, 64], F32, name="t12k", tag="t12k")
+            if n + K_SHIFT < NPAIR:
+                rk = q_rows(n + K_SHIFT)[2]
+                t12 = q_tile_of[n + K_SHIFT][3][:, :, rk : rk + 2, :]
+            else:
+                rope_tmp[n] = rope.tile([P, 2, 2, 64], F32, name="t12k", tag="t12k")
+                t12 = rope_tmp[n][:]
             bank = banks_of[n][2][:]
             nc.vector.tensor_tensor(
                 out=t12[:, 0],
@@ -327,11 +339,10 @@ def tile_diffucoderattention_pa_t_kernel(tc, hidden_states, Wq, Wk, Wv, out_0, o
                 in1=bank.rearrange("p (a s i e) -> p a s i e", a=2, s=4, e=2)[:, :, 0, :, ::-1],
                 op=ALU.mult,
             )
-            rope_tmp[("k", n)] = t12
 
         def rope_k_add(n, eng):
             ko, vo, k, grp = kv_tile_of[n]
-            t12 = rope_tmp[("k", n)]
+            t12 = rope_tmp[n]
             eng.tensor_tensor(
                 out=ko[:, 2 * k : 2 * k + 2, 0:64],
                 in0=t12[:, 0],
@@ -340,9 +351,9 @@ def tile_diffucoderattention_pa_t_kernel(tc, hidden_states, Wq, Wk, Wv, out_0, o
             )
 
         def copy_q(n):
-            qo, k, grp = q_tile_of[n]
+            r0, rq, rk = q_rows(n)
             nc.scalar.copy(
-                out=qo[:, 8 * k : 8 * k + 8, 64:128], in_=banks_of[n][1][:].rearrange("p (m f) -> p m f", m=8)
+                out=q_tile_of[n][0][:, r0 + rq : r0 + rq + 8, 64:128], in_=banks_of[n][1][:].rearrange("p (m f) -> p m f", m=8)
             )
 
         def copy_kv(n):
@@ -352,19 +363,35 @@ def tile_diffucoderattention_pa_t_kernel(tc, hidden_states, Wq, Wk, Wv, out_0, o
             copy(
                 out=vo[:, 2 * k : 2 * k + 2, :], in_=bank_k[:].rearrange("p (a s f) -> p a s f", a=2, s=2)[:, :, 1, :]
             )
+            if ko is None:
+                r0, rq, rk = q_rows(n + K_SHIFT)
+                ko, k = q_tile_of[n + K_SHIFT][0], (r0 + rk) // 2
             copy(
                 out=ko[:, 2 * k : 2 * k + 2, 64:128],
                 in_=bank_k[:].rearrange("p (a s f) -> p a s f", a=2, s=4)[:, :, 1, :],
             )
 
         def store_q(n):
-            qo, k, grp = q_tile_of[n]
+            qo, i, grp, t12 = q_tile_of[n]
             if grp[-1] != n:
                 return
             b, j0 = grp[0] // 4, 2 * (grp[0] % 4)
             dst = out_0[b].rearrange("(p j) h d -> p (j h d)", j=TPP)
             nc.sync.dma_start(
-                out=dst[:, j0 * 512 : (j0 + 2 * len(grp)) * 512], in_=qo[:].rearrange("p m d -> p (m d)")
+                out=dst[:, j0 * 512 : (j0 + 2 * len(grp)) * 512],
+                in_=qo[:, 2 : 2 + 8 * len(grp), :].rearrange("p m d -> p (m d)"),
+            )
+
+        def store_k_beside_q(n):
+            qo, i, grp, t12 = q_tile_of[n]
+            if grp[-1] != n or n < K_SHIFT:
+                return
+            j = grp[0] - K_SHIFT
+            b, j0 = j // 4, 2 * (j % 4)
+            dst = out_1[b].rearrange("(p j) o d -> p (j o d)", j=TPP)[:, j0 * P : (j0 + 2 * len(grp)) * P]
+            src = qo[:].rearrange("p (u m) d -> p u (m d)", m=2)
+            nc.sync.dma_start(
+                out=dst.rearrange("p (u x) -> p u x", u=len(grp)), in_=src[:, 0:10:9, :] if len(grp) == 2 else src[:, 0:1, :]
             )
 
         def store_kv(n, which):
@@ -393,20 +420,18 @@ def tile_diffucoderattention_pa_t_kernel(tc, hidden_states, Wq, Wk, Wv, out_0, o
         last = NPAIR - 1
         for n in range(NPAIR):
             j = n - K_LAG
-            q_out_tile(n)
+            if n < K_SHIFT:
+                q_out_tile(n)
             bank_r = psum.tile([P, 512], F32, name="bank_r", tag="bank_r")
             bank_p = psum.tile([P, 512], F32, name="bank_p", tag="bank_p")
             banks_of[n] = (bank_r, bank_p)
-            if j >= 1:
-                rope_k_add(j - 1, nc.gpsimd)
-                store_kv(j - 1, 0)
             mx(n, bank_r, 0)
             rope_q_mul(n)
             if n < FINE_FROM:
                 rope_q_add(n, nc.gpsimd)
             elif n < last:
-                rope_q_add(n, nc.gpsimd, 0, 4)
-                rope_q_add(n, nc.gpsimd, 4, 8)
+                rope_q_add(n, nc.gpsimd, 0, 6)
+                rope_q_add(n, nc.gpsimd, 6, 10)
             if n == 0:
                 ahead(2)
             mx(n, bank_p, 256)
@@ -423,18 +448,23 @@ def tile_diffucoderattention_pa_t_kernel(tc, hidden_states, Wq, Wk, Wv, out_0, o
             if n == 2:
                 quantise_w(0, 512, 768)
                 quantise_w(1, 512, 768)
+            if K_SHIFT <= n + 1 < NPAIR:
+                q_out_tile(n + 1)
             if j >= 0:
                 kv_passes(j)
                 rope_k_mul(j)
             if n < FINE_FROM:
                 store_q(n)
+                store_k_beside_q(n)
             elif n < last:
                 store_q_tile(n, 0)
+                store_k_beside_q(n)
                 store_q_tile(n, 1)
         kv_passes(last - 2)
         rope_k_mul(last - 2)
         rope_q_add(last, nc.vector)
         store_q(last)
+        store_k_beside_q(last)
         rope_k_add(last - 3, nc.gpsimd)
         rope_k_add(last - 2, nc.gpsimd)
         store_kv(last - 2, 0)

@@ -29,7 +29,6 @@ X_CHUNKS = [(0, 0, 2), (0, 2, 2), (0, 4, 2), (0, 6, 2), (1, 0, 4), (1, 4, 4), (2
 K_LAG = 3
 FINE_FROM = 13
 T_AHEAD = 3
-SORT_FROM = 7
 KV_VECTOR_TO = 9
 Q_GROUPS = [[0, 1], [2, 3], [4, 5], [6, 7], [8, 9], [10], [11], [12], [13], [14], [15]]
 K_SHIFT = 4
@@ -141,27 +140,11 @@ def tile_diffucoderattention_pa_t_kernel(tc, hidden_states, Wq, Wk, Wv, out_0, o
             banks = []
             for a in range(2):
                 tp = psum.tile([P, 4, P], F32, name="tp%d" % a, tag="tp%d" % a, bufs=1)
-                if a == 0 and n in sorted_of:
-                    for v in range(4):
-                        nc.tensor.transpose(tp[:, v, :], sorted_of[n][:, v, :], ident[:])
-                    banks.append(tp)
-                    continue
                 for v in range(4):
                     c0 = (off + a) * 512 + (v // 2) * 256 + v % 2
                     nc.tensor.transpose(tp[:, v, :], xw[:, c0 : c0 + 255 : 2], ident[:])
                 banks.append(tp)
             return banks
-
-        sorted_of = {}
-
-        def sort_words(n):
-            xt, off = x_of_pair[n]
-            so = work.tile([P, 4, P], F32, name="so", tag="so", bufs=3)
-            nc.scalar.copy(
-                out=so[:].rearrange("p (g u) r -> p g u r", u=2),
-                in_=xt[:, off * E : (off + 1) * E].bitcast(F32).rearrange("p (g r u) -> p g u r", g=2, u=2),
-            )
-            sorted_of[n] = so
 
         def evacuate(banks):
             xg = work.tile([P, 2048], BF16, name="xg", tag="xg", align_bytes=64)
@@ -436,8 +419,6 @@ def tile_diffucoderattention_pa_t_kernel(tc, hidden_states, Wq, Wk, Wv, out_0, o
                 ahead(2)
             mx(n, bank_p, 256)
             copy_q(n)
-            if SORT_FROM <= n + T_AHEAD + 1 < NPAIR:
-                sort_words(n + T_AHEAD + 1)
             ahead(n + T_AHEAD)
             if n + 2 < NPAIR:
                 xq_of[n + 2] = quantise_x(xg_of[n + 2])

@@ -98,19 +98,16 @@ def tile_diffucoderattention_pa_t_kernel(tc, hidden_states, Wq, Wk, Wv, out_0, o
         turns = const.tile([P, NT], F32, name="turns")
         red1 = const.tile([P, NT], F32, name="red1")
         red = const.tile([P, NT], F32, name="red")
-        nabs = const.tile([P, NT], F32, name="nabs")
+        red_pm = const.tile([P, NT, 2], F32, name="red_pm")
+        absr = const.tile([P, NT], F32, name="absr")
         carg = const.tile([P, NT], F32, name="carg")
-        sin_h = const.tile([P, NT], F32, name="sin_h")
-        cos_h = const.tile([P, NT], F32, name="cos_h")
-        sq_h = const.tile([P, NT], F32, name="sq_h")
-        sin_half = const.tile([P, NT], F32, name="sin_half")
         sign2 = const.tile([P, 2], F32, name="sign2")
         tab = const.tile([P, 4, 2, 2, 64], F32, name="tab")
 
         nc.vector.tensor_copy(out=pos_f[:], in_=pos_i[:])
         nc.vector.memset(freq[:, 0:1], 1.0)
-        nc.vector.memset(sign2[:, 0:1], -2.0)
-        nc.vector.memset(sign2[:, 1:2], 2.0)
+        nc.vector.memset(sign2[:, 0:1], -1.0)
+        nc.vector.memset(sign2[:, 1:2], 1.0)
         w = 1
         while w < 32:
             nc.vector.tensor_scalar(
@@ -123,15 +120,19 @@ def tile_diffucoderattention_pa_t_kernel(tc, hidden_states, Wq, Wk, Wv, out_0, o
             in1=freq[:].unsqueeze(1).to_broadcast([P, TPP, 32]),
             op=ALU.mult,
         )
-        nc.vector.tensor_scalar(
-            out=turns_i[:], in0=ang[:], scalar1=1.0 / TWO_PI, scalar2=0.25, op0=ALU.mult, op1=ALU.add
-        )
+        nc.vector.tensor_scalar(out=turns_i[:], in0=ang[:], scalar1=1.0 / TWO_PI, scalar2=None, op0=ALU.mult)
         nc.vector.tensor_copy(out=turns[:], in_=turns_i[:])
         nc.vector.scalar_tensor_tensor(out=red1[:], in0=turns[:], scalar=-C1, in1=ang[:], op0=ALU.mult, op1=ALU.add)
         nc.vector.scalar_tensor_tensor(out=red[:], in0=turns[:], scalar=-C2, in1=red1[:], op0=ALU.mult, op1=ALU.add)
-        nc.vector.scalar_tensor_tensor(out=nabs[:], in0=red[:], scalar=-1.0, in1=red[:], op0=ALU.mult, op1=ALU.min)
+        nc.scalar.activation(out=absr[:], in_=red[:], func=ACT.Abs)
+        nc.vector.tensor_tensor(
+            out=red_pm[:],
+            in0=red[:].unsqueeze(2).to_broadcast([P, NT, 2]),
+            in1=sign2[:].unsqueeze(1).to_broadcast([P, NT, 2]),
+            op=ALU.mult,
+        )
         nc.vector.tensor_scalar(
-            out=carg[:], in0=nabs[:], scalar1=0.5, scalar2=0.5 * math.pi, op0=ALU.mult, op1=ALU.add
+            out=carg[:], in0=absr[:], scalar1=-1.0, scalar2=0.5 * math.pi, op0=ALU.mult, op1=ALU.add
         )
 
         def transposes(n):
@@ -187,30 +188,22 @@ def tile_diffucoderattention_pa_t_kernel(tc, hidden_states, Wq, Wk, Wv, out_0, o
                 in_=wg_v[:, g, c0:c1, :].rearrange("p c t -> p (c t)"),
             )
 
-        def tab_sin():
-            nc.vector.tensor_tensor(
-                out=tab[:, :, 1].rearrange("p q a (i e) -> p q (a i) e", e=2),
-                in0=sin_half[:].rearrange("p (q x) -> p q x", q=4).unsqueeze(3).to_broadcast([P, 4, 64, 2]),
-                in1=sign2[:].unsqueeze(1).unsqueeze(1).to_broadcast([P, 4, 64, 2]),
-                op=ALU.mult,
+        def tables():
+            nc.scalar.activation(
+                out=tab[:, :, 1].rearrange("p q a f -> p q (a f)"),
+                in_=red_pm[:].rearrange("p (q x) e -> p q (x e)", q=4),
+                func=ACT.Sin,
             )
-
-        def tab_cos():
-            nc.vector.tensor_scalar(
+            nc.scalar.activation(
                 out=tab[:, :, 0].rearrange("p q a (i e) -> p q (a i) e", e=2),
-                in0=sq_h[:].rearrange("p (q x) -> p q x", q=4).unsqueeze(3).to_broadcast([P, 4, 64, 2]),
-                scalar1=-2.0,
-                scalar2=1.0,
-                op0=ALU.mult,
-                op1=ALU.add,
+                in_=carg[:].rearrange("p (q x) -> p q x", q=4).unsqueeze(3).to_broadcast([P, 4, 64, 2]),
+                func=ACT.Sin,
             )
 
         xg_of[0] = evacuate(transposes(0))
-        nc.scalar.activation(out=sin_h[:], in_=red[:], func=ACT.Sin, scale=0.5)
-        nc.scalar.activation(out=cos_h[:], in_=carg[:], func=ACT.Sin)
-        nc.scalar.activation(out=sq_h[:], in_=sin_h[:], func=ACT.Square)
         regroup_q(nc.vector.tensor_copy, 0, 0)
         regroup_q(nc.scalar.copy, 0, 1)
+        tables()
         xq_of[0] = quantise_x(xg_of[0])
         regroup_q(nc.vector.tensor_copy, 1, 0)
         quantise_w(0, 0, 256)
@@ -220,9 +213,6 @@ def tile_diffucoderattention_pa_t_kernel(tc, hidden_states, Wq, Wk, Wv, out_0, o
         quantise_w(1, 256, 512)
         xg_of[1] = evacuate(transposes(1))
         xq_of[1] = quantise_x(xg_of[1])
-        nc.vector.tensor_tensor(out=sin_half[:], in0=sin_h[:], in1=cos_h[:], op=ALU.mult)
-        tab_sin()
-        tab_cos()
 
         banks_of = {}
         q_tile_of = {}

@@ -27,9 +27,9 @@ C2 = TWO_PI - C1
 
 X_CHUNKS = [(0, 0, 2), (0, 2, 2), (0, 4, 2), (0, 6, 2), (1, 0, 4), (1, 4, 4), (2, 0, 4), (2, 4, 4), (3, 0, 4), (3, 4, 4)]
 K_LAG = 3
-FINE_FROM = 13
+FINE_FROM = 12
 T_AHEAD = 3
-KV_VECTOR_TO = 9
+KV_VECTOR_TO = 8
 Q_GROUPS = [[0, 1], [2, 3], [4, 5], [6, 7], [8, 9], [10], [11], [12], [13], [14], [15]]
 K_SHIFT = 4
 KV_GROUPS = [[0, 1], [2, 3], [4, 5], [6, 7], [8, 9], [10, 11], [12, 13], [14, 15]]
@@ -95,7 +95,6 @@ def tile_diffucoderattention_pa_t_kernel(tc, hidden_states, Wq, Wk, Wv, out_0, o
         freq = const.tile([P, 32], F32, name="freq")
         ang = const.tile([P, NT], F32, name="ang")
         turns_i = const.tile([P, NT], I32, name="turns_i")
-        turns = const.tile([P, NT], F32, name="turns")
         red1 = const.tile([P, NT], F32, name="red1")
         red = const.tile([P, NT], F32, name="red")
         red_pm = const.tile([P, NT, 2], F32, name="red_pm")
@@ -108,22 +107,29 @@ def tile_diffucoderattention_pa_t_kernel(tc, hidden_states, Wq, Wk, Wv, out_0, o
         nc.vector.memset(freq[:, 0:1], 1.0)
         nc.vector.memset(sign2[:, 0:1], -1.0)
         nc.vector.memset(sign2[:, 1:2], 1.0)
-        w = 1
+        for i in range(1, 4):
+            nc.vector.tensor_scalar(
+                out=freq[:, i : i + 1], in0=freq[:, 0:1], scalar1=THETA ** (-i / 32.0), scalar2=None, op0=ALU.mult
+            )
+        w = 4
         while w < 32:
             nc.vector.tensor_scalar(
                 out=freq[:, w : 2 * w], in0=freq[:, 0:w], scalar1=THETA ** (-w / 32.0), scalar2=None, op0=ALU.mult
             )
             w *= 2
-        nc.vector.tensor_tensor(
-            out=ang[:].rearrange("p (j i) -> p j i", j=TPP),
-            in0=pos_f[:].unsqueeze(2).to_broadcast([P, TPP, 32]),
-            in1=freq[:].unsqueeze(1).to_broadcast([P, TPP, 32]),
-            op=ALU.mult,
+        pos_b = pos_f[:].unsqueeze(2).to_broadcast([P, TPP, 32])
+        freq_b = freq[:].unsqueeze(1).to_broadcast([P, TPP, 32])
+        nc.vector.scalar_tensor_tensor(
+            out=turns_i[:].rearrange("p (j i) -> p j i", j=TPP),
+            in0=pos_b,
+            scalar=1.0 / TWO_PI,
+            in1=freq_b,
+            op0=ALU.mult,
+            op1=ALU.mult,
         )
-        nc.vector.tensor_scalar(out=turns_i[:], in0=ang[:], scalar1=1.0 / TWO_PI, scalar2=None, op0=ALU.mult)
-        nc.vector.tensor_copy(out=turns[:], in_=turns_i[:])
-        nc.vector.scalar_tensor_tensor(out=red1[:], in0=turns[:], scalar=-C1, in1=ang[:], op0=ALU.mult, op1=ALU.add)
-        nc.vector.scalar_tensor_tensor(out=red[:], in0=turns[:], scalar=-C2, in1=red1[:], op0=ALU.mult, op1=ALU.add)
+        nc.vector.tensor_tensor(out=ang[:].rearrange("p (j i) -> p j i", j=TPP), in0=pos_b, in1=freq_b, op=ALU.mult)
+        nc.vector.scalar_tensor_tensor(out=red1[:], in0=turns_i[:], scalar=-C1, in1=ang[:], op0=ALU.mult, op1=ALU.add)
+        nc.vector.scalar_tensor_tensor(out=red[:], in0=turns_i[:], scalar=-C2, in1=red1[:], op0=ALU.mult, op1=ALU.add)
         nc.scalar.activation(out=absr[:], in_=red[:], func=ACT.Abs)
         nc.vector.tensor_tensor(
             out=red_pm[:],
@@ -257,20 +263,21 @@ def tile_diffucoderattention_pa_t_kernel(tc, hidden_states, Wq, Wk, Wv, out_0, o
 
         rope_tmp = {}
 
-        def rope_q_mul(n):
+        def rope_q_mul(n, a0=0, na=2):
             r0, rq, rk = q_rows(n)
-            t12 = q_tile_of[n][3][:, :, rq : rq + 8, :].rearrange("p c (a h) f -> p c a h f", a=2)
-            bank = banks_of[n][0][:]
+            t12 = q_tile_of[n][3][:, :, rq : rq + 8, :].rearrange("p c (a h) f -> p c a h f", a=2)[:, :, a0 : a0 + na]
+            bank = banks_of[n][0][:, a0 * 256 : (a0 + na) * 256]
+            tb = tab[:, n % 4, :, a0 : a0 + na]
             nc.vector.tensor_tensor(
                 out=t12[:, 0],
-                in0=tab[:, n % 4, 0].unsqueeze(2).to_broadcast([P, 2, 4, 64]),
-                in1=bank.rearrange("p (a h f) -> p a h f", a=2, h=4),
+                in0=tb[:, 0].unsqueeze(2).to_broadcast([P, na, 4, 64]),
+                in1=bank.rearrange("p (a h f) -> p a h f", a=na, h=4),
                 op=ALU.mult,
             )
             nc.vector.tensor_tensor(
                 out=t12[:, 1].rearrange("p a h (i e) -> p a h i e", e=2),
-                in0=tab[:, n % 4, 1].rearrange("p a (i e) -> p a i e", e=2).unsqueeze(2).to_broadcast([P, 2, 4, 32, 2]),
-                in1=bank.rearrange("p (a h i e) -> p a h i e", a=2, h=4, e=2)[:, :, :, :, ::-1],
+                in0=tb[:, 1].rearrange("p a (i e) -> p a i e", e=2).unsqueeze(2).to_broadcast([P, na, 4, 32, 2]),
+                in1=bank.rearrange("p (a h i e) -> p a h i e", a=na, h=4, e=2)[:, :, :, :, ::-1],
                 op=ALU.mult,
             )
 
@@ -297,7 +304,7 @@ def tile_diffucoderattention_pa_t_kernel(tc, hidden_states, Wq, Wk, Wv, out_0, o
                 rk = q_rows(n + K_SHIFT)[2]
                 t12 = q_tile_of[n + K_SHIFT][3][:, :, rk : rk + 2, :]
             else:
-                rope_tmp[n] = rope.tile([P, 2, 2, 64], F32, name="t12k", tag="t12k")
+                rope_tmp[n] = rope.tile([P, 2, 2, 64], F32, name="t12k", tag="t12k", bufs=4)
                 t12 = rope_tmp[n][:]
             bank = banks_of[n][2][:]
             nc.vector.tensor_tensor(
@@ -387,7 +394,12 @@ def tile_diffucoderattention_pa_t_kernel(tc, hidden_states, Wq, Wk, Wv, out_0, o
             bank_k = psum.tile([P, 512], F32, name="bank_k", tag=tag, bufs=(2 if tag == "bank_k" else 1))
             banks_of[j] = banks_of[j][:2] + (bank_k,)
             mx(j, bank_k, 512)
-            copy_kv(j)
+            if j > KV_VECTOR_TO:
+                rope_k_mul(j)
+                copy_kv(j)
+            else:
+                copy_kv(j)
+                rope_k_mul(j)
             store_kv(j, 1)
 
         last = NPAIR - 1
@@ -399,18 +411,21 @@ def tile_diffucoderattention_pa_t_kernel(tc, hidden_states, Wq, Wk, Wv, out_0, o
             bank_p = psum.tile([P, 512], F32, name="bank_p", tag="bank_p")
             banks_of[n] = (bank_r, bank_p)
             mx(n, bank_r, 0)
-            rope_q_mul(n)
             if n < FINE_FROM:
+                rope_q_mul(n)
                 rope_q_add(n, nc.gpsimd)
-            elif n < last:
-                rope_q_add(n, nc.gpsimd, 0, 6)
-                rope_q_add(n, nc.gpsimd, 6, 10)
+            else:
+                for a in range(2):
+                    rope_q_mul(n, a, 1)
+                    if a == 0 and n + 2 < NPAIR:
+                        xq_of[n + 2] = quantise_x(xg_of[n + 2])
+                    rope_q_add(n, nc.gpsimd, 6 * a, 6 + 4 * a)
             if n == 0:
                 ahead(2)
             mx(n, bank_p, 256)
             copy_q(n)
             ahead(n + T_AHEAD)
-            if n + 2 < NPAIR:
+            if n < FINE_FROM and n + 2 < NPAIR:
                 xq_of[n + 2] = quantise_x(xg_of[n + 2])
             if n == 0:
                 regroup_kv(wk_raw, 512)
@@ -423,26 +438,19 @@ def tile_diffucoderattention_pa_t_kernel(tc, hidden_states, Wq, Wk, Wv, out_0, o
                 q_out_tile(n + 1)
             if j >= 0:
                 kv_passes(j)
-                rope_k_mul(j)
             if n < FINE_FROM:
                 store_q(n)
                 store_k_beside_q(n)
-            elif n < last:
+            else:
                 store_q_tile(n, 0)
                 store_k_beside_q(n)
                 store_q_tile(n, 1)
         kv_passes(last - 2)
-        rope_k_mul(last - 2)
-        rope_q_add(last, nc.vector)
-        store_q(last)
-        store_k_beside_q(last)
         rope_k_add(last - 3, nc.gpsimd)
         rope_k_add(last - 2, nc.gpsimd)
         store_kv(last - 2, 0)
         kv_passes(last - 1, "tp0")
-        rope_k_mul(last - 1)
         kv_passes(last, "tp1")
-        rope_k_mul(last)
         rope_k_add(last - 1, nc.vector)
         rope_k_add(last, nc.vector)
         store_kv(last, 0)

@@ -29,6 +29,7 @@ X_CHUNKS = [(0, 0, 2), (0, 2, 2), (0, 4, 2), (0, 6, 2), (1, 0, 4), (1, 4, 4), (2
 K_LAG = 3
 FINE_FROM = 12
 T_AHEAD = 3
+SORT_FROM = 7
 KV_VECTOR_TO = 8
 Q_GROUPS = [[0, 1], [2, 3], [4, 5], [6, 7], [8, 9], [10], [11], [12], [13], [14], [15]]
 K_SHIFT = 4
@@ -68,7 +69,6 @@ def tile_diffucoderattention_pa_t_kernel(tc, hidden_states, Wq, Wk, Wv, out_0, o
             nc.sync.dma_start(out=wq_raw[g][:], in_=wq_view[g])
         load_x(1)
         load_x(2)
-        load_x(3)
         nc.sync.dma_start(
             out=wk_raw[:].rearrange("p (g x) -> p g x", g=2),
             in_=Wk.rearrange("(g q t) c -> q g (t c)", g=2, q=P, t=4),
@@ -77,7 +77,7 @@ def tile_diffucoderattention_pa_t_kernel(tc, hidden_states, Wq, Wk, Wv, out_0, o
             out=wv_raw[:].rearrange("p (g x) -> p g x", g=2),
             in_=Wv.rearrange("(g q t) c -> q g (t c)", g=2, q=P, t=4),
         )
-        for ci in range(4, len(X_CHUNKS)):
+        for ci in range(3, len(X_CHUNKS)):
             load_x(ci)
 
         pos_i = const.tile([P, TPP], I32, name="pos_i")
@@ -147,11 +147,27 @@ def tile_diffucoderattention_pa_t_kernel(tc, hidden_states, Wq, Wk, Wv, out_0, o
             banks = []
             for a in range(2):
                 tp = psum.tile([P, 4, P], F32, name="tp%d" % a, tag="tp%d" % a, bufs=1)
+                if a == 0 and n in sorted_of:
+                    for v in range(4):
+                        nc.tensor.transpose(tp[:, v, :], sorted_of[n][:, v, :], ident[:])
+                    banks.append(tp)
+                    continue
                 for v in range(4):
                     c0 = (off + a) * 512 + (v // 2) * 256 + v % 2
                     nc.tensor.transpose(tp[:, v, :], xw[:, c0 : c0 + 255 : 2], ident[:])
                 banks.append(tp)
             return banks
+
+        sorted_of = {}
+
+        def sort_words(n):
+            xt, off = x_of_pair[n]
+            so = work.tile([P, 4, P], F32, name="so", tag="so", bufs=3)
+            nc.vector.tensor_copy(
+                out=so[:].rearrange("p (g u) r -> p g u r", u=2),
+                in_=xt[:, off * E : (off + 1) * E].bitcast(F32).rearrange("p (g r u) -> p g u r", g=2, u=2),
+            )
+            sorted_of[n] = so
 
         def evacuate(banks):
             xg = work.tile([P, 2048], BF16, name="xg", tag="xg", align_bytes=64)
@@ -182,7 +198,7 @@ def tile_diffucoderattention_pa_t_kernel(tc, hidden_states, Wq, Wk, Wv, out_0, o
             )
 
         def regroup_kv(raw, c0):
-            nc.scalar.copy(
+            nc.vector.tensor_copy(
                 out=wg_v[:, :, c0 : c0 + P, :].rearrange("p g (c i) t -> p g c t i", i=4),
                 in_=raw[:].rearrange("p (g t c i) -> p g c t i", g=2, t=4, i=4),
             )
@@ -219,6 +235,8 @@ def tile_diffucoderattention_pa_t_kernel(tc, hidden_states, Wq, Wk, Wv, out_0, o
         quantise_w(1, 256, 512)
         xg_of[1] = evacuate(transposes(1))
         xq_of[1] = quantise_x(xg_of[1])
+        regroup_kv(wk_raw, 512)
+        regroup_kv(wv_raw, 640)
 
         banks_of = {}
         q_tile_of = {}
@@ -274,6 +292,8 @@ def tile_diffucoderattention_pa_t_kernel(tc, hidden_states, Wq, Wk, Wv, out_0, o
                 in1=bank.rearrange("p (a h f) -> p a h f", a=na, h=4),
                 op=ALU.mult,
             )
+            if SORT_FROM <= n + T_AHEAD + 1 < NPAIR and a0 == 0 and n % 2 == 0:
+                sort_words(n + T_AHEAD + 1)
             nc.vector.tensor_tensor(
                 out=t12[:, 1].rearrange("p a h (i e) -> p a h i e", e=2),
                 in0=tb[:, 1].rearrange("p a (i e) -> p a i e", e=2).unsqueeze(2).to_broadcast([P, na, 4, 32, 2]),
@@ -340,7 +360,7 @@ def tile_diffucoderattention_pa_t_kernel(tc, hidden_states, Wq, Wk, Wv, out_0, o
             bank_k = banks_of[n][2]
             ko, vo, k, grp = kv_tile_of[n]
             copy = nc.vector.tensor_copy if n <= KV_VECTOR_TO else nc.scalar.copy
-            copy(
+            nc.scalar.copy(
                 out=vo[:, 2 * k : 2 * k + 2, :], in_=bank_k[:].rearrange("p (a s f) -> p a s f", a=2, s=2)[:, :, 1, :]
             )
             if ko is None:
@@ -427,11 +447,7 @@ def tile_diffucoderattention_pa_t_kernel(tc, hidden_states, Wq, Wk, Wv, out_0, o
             ahead(n + T_AHEAD)
             if n < FINE_FROM and n + 2 < NPAIR:
                 xq_of[n + 2] = quantise_x(xg_of[n + 2])
-            if n == 0:
-                regroup_kv(wk_raw, 512)
             if n == 1:
-                regroup_kv(wv_raw, 640)
-            if n == 2:
                 quantise_w(0, 512, 768)
                 quantise_w(1, 512, 768)
             if K_SHIFT <= n + 1 < NPAIR:

import math
from contextlib import ExitStack

import concourse.mybir as mybir
from concourse.masks import make_identity

FLOPS = 2 * 4096 * 1024 * 768

F32 = mybir.dt.float32
BF16 = mybir.dt.bfloat16
I32 = mybir.dt.int32
U32 = mybir.dt.uint32
U8 = mybir.dt.uint8
FP8X4 = mybir.dt.float8_e4m3fn_x4
ALU = mybir.AluOpType
ACT = mybir.ActivationFunctionType

P = 128
NB = 4
TPP = 8
E = 1024
NPAIR = 16
THETA = 10000.0
TWO_PI = 2.0 * math.pi
C1 = 51472.0 / 8192.0
C2 = TWO_PI - C1

X_CHUNKS = [(0, 0, 2), (0, 2, 2), (0, 4, 2), (0, 6, 2), (1, 0, 4), (1, 4, 4), (2, 0, 4), (2, 4, 4), (3, 0, 4), (3, 4, 4)]
K_LAG = 3
FINE_FROM = 12
T_AHEAD = 3
SORT_FROM = 7
KV_VECTOR_TO = 8
Q_GROUPS = [[0, 1], [2, 3], [4, 5], [6, 7], [8, 9], [10], [11], [12], [13], [14], [15]]
K_SHIFT = 4
KV_GROUPS = [[0, 1], [2, 3], [4, 5], [6, 7], [8, 9], [10, 11], [12, 13], [14, 15]]


def tile_diffucoderattention_pa_t_kernel(tc, hidden_states, Wq, Wk, Wv, out_0, out_1, out_2):
    nc = tc.nc
    with ExitStack() as ctx:
        const = ctx.enter_context(tc.tile_pool(name="const", bufs=1))
        xin = ctx.enter_context(tc.tile_pool(name="xin", bufs=1))
        work = ctx.enter_context(tc.tile_pool(name="work", bufs=4))
        rope = ctx.enter_context(tc.tile_pool(name="rope", bufs=3))
        outp = ctx.enter_context(tc.tile_pool(name="outp", bufs=4))
        psum = ctx.enter_context(tc.psum_pool(name="psum", bufs=2))
        ctx.enter_context(tc.manual_schedule())

        wq_raw = [const.tile([P, 2048], BF16, name="wq_raw%d" % g) for g in range(2)]
        wk_raw = const.tile([P, 1024], BF16, name="wk_raw")
        wv_raw = const.tile([P, 1024], BF16, name="wv_raw")
        wq_view = Wq.rearrange("(g q t) c -> g q (t c)", g=2, q=P, t=4)
        x_tiles = []
        x_of_pair = {}
        for ci, (b, j0, nj) in enumerate(X_CHUNKS):
            xt = xin.tile([P, nj * E], BF16, name="x%d" % ci)
            x_tiles.append(xt)
            for k in range(nj // 2):
                x_of_pair[b * 4 + j0 // 2 + k] = (xt, 2 * k)

        def load_x(ci):
            b, j0, nj = X_CHUNKS[ci]
            src = hidden_states[b].rearrange("(p j) e -> p (j e)", j=TPP)
            nc.sync.dma_start(out=x_tiles[ci][:], in_=src[:, j0 * E : (j0 + nj) * E])

        load_x(0)
        for g in range(2):
            nc.sync.dma_start(out=wq_raw[g][:], in_=wq_view[g])
        load_x(1)
        load_x(2)
        nc.sync.dma_start(
            out=wk_raw[:].rearrange("p (g x) -> p g x", g=2),
            in_=Wk.rearrange("(g q t) c -> q g (t c)", g=2, q=P, t=4),
        )
        nc.sync.dma_start(
            out=wv_raw[:].rearrange("p (g x) -> p g x", g=2),
            in_=Wv.rearrange("(g q t) c -> q g (t c)", g=2, q=P, t=4),
        )
        for ci in range(3, len(X_CHUNKS)):
            load_x(ci)

        pos_i = const.tile([P, TPP], I32, name="pos_i")
        nc.gpsimd.iota(pos_i[:], pattern=[[1, TPP]], base=0, channel_multiplier=TPP)
        ident = const.tile([P, P], F32, name="ident")
        make_identity(nc, ident[:])

        zero1 = const.tile([P, 1], F32, name="zero1")
        warm = const.tile([P, 1], F32, name="warm")
        nc.vector.memset(zero1[:], 0.0)
        nc.scalar.activation(out=warm[:], in_=zero1[:], func=ACT.Sin)

        NT = TPP * 32
        pos_f = const.tile([P, TPP], F32, name="pos_f")
        freq = const.tile([P, 32], F32, name="freq")
        ang = const.tile([P, NT], F32, name="ang")
        turns_i = const.tile([P, NT], I32, name="turns_i")
        red1 = const.tile([P, NT], F32, name="red1")
        red = const.tile([P, NT], F32, name="red")
        red_pm = const.tile([P, NT, 2], F32, name="red_pm")
        absr = const.tile([P, NT], F32, name="absr")
        carg = const.tile([P, NT], F32, name="carg")
        sign2 = const.tile([P, 2], F32, name="sign2")
        tab = const.tile([P, 4, 2, 2, 64], F32, name="tab")

        nc.vector.tensor_copy(out=pos_f[:], in_=pos_i[:])
        nc.vector.memset(freq[:, 0:1], 1.0)
        nc.vector.memset(sign2[:, 0:1], -1.0)
        nc.vector.memset(sign2[:, 1:2], 1.0)
        for i in range(1, 4):
            nc.vector.tensor_scalar(
                out=freq[:, i : i + 1], in0=freq[:, 0:1], scalar1=THETA ** (-i / 32.0), scalar2=None, op0=ALU.mult
            )
        w = 4
        while w < 32:
            nc.vector.tensor_scalar(
                out=freq[:, w : 2 * w], in0=freq[:, 0:w], scalar1=THETA ** (-w / 32.0), scalar2=None, op0=ALU.mult
            )
            w *= 2
        pos_b = pos_f[:].unsqueeze(2).to_broadcast([P, TPP, 32])
        freq_b = freq[:].unsqueeze(1).to_broadcast([P, TPP, 32])
        nc.vector.scalar_tensor_tensor(
            out=turns_i[:].rearrange("p (j i) -> p j i", j=TPP),
            in0=pos_b,
            scalar=1.0 / TWO_PI,
            in1=freq_b,
            op0=ALU.mult,
            op1=ALU.mult,
        )
        nc.vector.tensor_tensor(out=ang[:].rearrange("p (j i) -> p j i", j=TPP), in0=pos_b, in1=freq_b, op=ALU.mult)
        nc.vector.scalar_tensor_tensor(out=red1[:], in0=turns_i[:], scalar=-C1, in1=ang[:], op0=ALU.mult, op1=ALU.add)
        nc.vector.scalar_tensor_tensor(out=red[:], in0=turns_i[:], scalar=-C2, in1=red1[:], op0=ALU.mult, op1=ALU.add)
        nc.scalar.activation(out=absr[:], in_=red[:], func=ACT.Abs)
        nc.vector.tensor_tensor(
            out=red_pm[:],
            in0=red[:].unsqueeze(2).to_broadcast([P, NT, 2]),
            in1=sign2[:].unsqueeze(1).to_broadcast([P, NT, 2]),
            op=ALU.mult,
        )
        nc.vector.tensor_scalar(
            out=carg[:], in0=absr[:], scalar1=-1.0, scalar2=0.5 * math.pi, op0=ALU.mult, op1=ALU.add
        )

        def transposes(n):
            xt, off = x_of_pair[n]
            xw = xt[:].bitcast(F32)
            banks = []
            for a in range(2):
                tp = psum.tile([P, 4, P], F32, name="tp%d" % a, tag="tp%d" % a, bufs=1)
                if a == 0 and n in sorted_of:
                    for v in range(4):
                        nc.tensor.transpose(tp[:, v, :], sorted_of[n][:, v, :], ident[:])
                    banks.append(tp)
                    continue
                for v in range(4):
                    c0 = (off + a) * 512 + (v // 2) * 256 + v % 2
                    nc.tensor.transpose(tp[:, v, :], xw[:, c0 : c0 + 255 : 2], ident[:])
                banks.append(tp)
            return banks

        sorted_of = {}

        def sort_words(n):
            xt, off = x_of_pair[n]
            so = work.tile([P, 4, P], F32, name="so", tag="so", bufs=3)
            nc.vector.tensor_copy(
                out=so[:].rearrange("p (g u) r -> p g u r", u=2),
                in_=xt[:, off * E : (off + 1) * E].bitcast(F32).rearrange("p (g r u) -> p g u r", g=2, u=2),
            )
            sorted_of[n] = so

        def evacuate(banks):
            xg = work.tile([P, 2048], BF16, name="xg", tag="xg", align_bytes=64)
            xgw = xg[:].bitcast(F32).rearrange("p (a g r u) -> p a g r u", a=2, g=2, r=P, u=2)
            for a in range(2):
                nc.scalar.copy(out=xgw[:, a], in_=banks[a][:].rearrange("p (g u) r -> p g r u", u=2))
            return xg

        def quantise_x(xg):
            xc = work.tile([P, 512], U32, name="xc", tag="xc", align_bytes=64, bufs=7)
            xs = work.tile([P, 512], U8, name="xs", tag="xs", align_bytes=64, bufs=7)
            nc.vector.quantize_mx(out=xc[:].bitcast(FP8X4), scales=xs[:], in_=xg[:])
            return xc, xs

        xg_of = {}
        xq_of = {}

        wg = const.tile([P, 2 * 768 * 4], BF16, name="wg", align_bytes=64)
        wg_v = wg[:].rearrange("p (g c t) -> p g c t", g=2, c=768, t=4)
        wc = const.tile([P, 2, 768], U32, name="wc", align_bytes=64)
        ws = const.tile([P, 2, 768], U8, name="ws", align_bytes=64)

        def regroup_q(copy, g, s):
            src = wq_raw[g][:].rearrange("p (t h s c i) -> p s h c t i", t=4, h=4, s=2, c=16, i=4)
            copy(
                out=wg_v[:, g, s * 256 : (s + 1) * 256, :].rearrange("p (h c i) t -> p h c t i", h=4, i=4),
                in_=src[:, s],
            )

        def regroup_kv(raw, c0):
            nc.vector.tensor_copy(
                out=wg_v[:, :, c0 : c0 + P, :].rearrange("p g (c i) t -> p g c t i", i=4),
                in_=raw[:].rearrange("p (g t c i) -> p g c t i", g=2, t=4, i=4),
            )

        def quantise_w(g, c0, c1):
            nc.vector.quantize_mx(
                out=wc[:, g, c0:c1].bitcast(FP8X4),
                scales=ws[:, g, c0:c1],
                in_=wg_v[:, g, c0:c1, :].rearrange("p c t -> p (c t)"),
            )

        def tables():
            nc.scalar.activation(
                out=tab[:, :, 1].rearrange("p q a f -> p q (a f)"),
                in_=red_pm[:].rearrange("p (q x) e -> p q (x e)", q=4),
                func=ACT.Sin,
            )
            nc.scalar.activation(
                out=tab[:, :, 0].rearrange("p q a (i e) -> p q (a i) e", e=2),
                in_=carg[:].rearrange("p (q x) -> p q x", q=4).unsqueeze(3).to_broadcast([P, 4, 64, 2]),
                func=ACT.Sin,
            )

        xg_of[0] = evacuate(transposes(0))
        regroup_q(nc.vector.tensor_copy, 0, 0)
        regroup_q(nc.scalar.copy, 0, 1)
        tables()
        xq_of[0] = quantise_x(xg_of[0])
        regroup_q(nc.vector.tensor_copy, 1, 0)
        quantise_w(0, 0, 256)
        quantise_w(1, 0, 256)
        regroup_q(nc.vector.tensor_copy, 1, 1)
        quantise_w(0, 256, 512)
        quantise_w(1, 256, 512)
        xg_of[1] = evacuate(transposes(1))
        xq_of[1] = quantise_x(xg_of[1])
        regroup_kv(wk_raw, 512)
        regroup_kv(wv_raw, 640)

        banks_of = {}
        q_tile_of = {}
        kv_tile_of = {}

        def mx(n, bank, c0):
            xc, xs = xq_of[n]
            for a in range(2):
                for g in range(2):
                    blk = slice((a * 2 + g) * P, (a * 2 + g + 1) * P)
                    nc.tensor.matmul_mx(
                        out=bank[:, a * 256 : (a + 1) * 256],
                        lhsT=xc[:, blk].bitcast(FP8X4),
                        lhsT_scale=xs[:, blk],
                        rhs=wc[:, g, c0 : c0 + 256].bitcast(FP8X4),
                        rhs_scale=ws[:, g, c0 : c0 + 256],
                        start=(g == 0),
                        stop=(g == 1),
                    )

        def q_rows(n):
            qo, i, grp, t12 = q_tile_of[n]
            return (10 * i, 2, 0) if i == 0 else (10 * i, 0, 8)

        def q_out_tile(n):
            for grp in Q_GROUPS:
                if grp[0] == n:
                    qo = outp.tile([P, len(grp) * 10, P], F32, name="qo", tag="qo")
                    for i, m in enumerate(grp):
                        q_tile_of[m] = [qo, i, grp, None]
            q_tile_of[n][3] = rope.tile([P, 2, 10, 64], F32, name="t12q", tag="t12q")

        def kv_out_tiles(n):
            for grp in KV_GROUPS:
                if grp[0] == n:
                    ko = None
                    if n + K_SHIFT >= NPAIR:
                        ko = outp.tile([P, len(grp) * 2, P], F32, name="ko", tag="ko", bufs=2)
                    vo = outp.tile([P, len(grp) * 2, P], F32, name="vo", tag="vo", bufs=6)
                    for k, m in enumerate(grp):
                        kv_tile_of[m] = (ko, vo, k, grp)

        rope_tmp = {}

        def rope_q_mul(n, a0=0, na=2):
            r0, rq, rk = q_rows(n)
            t12 = q_tile_of[n][3][:, :, rq : rq + 8, :].rearrange("p c (a h) f -> p c a h f", a=2)[:, :, a0 : a0 + na]
            bank = banks_of[n][0][:, a0 * 256 : (a0 + na) * 256]
            tb = tab[:, n % 4, :, a0 : a0 + na]
            nc.vector.tensor_tensor(
                out=t12[:, 0],
                in0=tb[:, 0].unsqueeze(2).to_broadcast([P, na, 4, 64]),
                in1=bank.rearrange("p (a h f) -> p a h f", a=na, h=4),
                op=ALU.mult,
            )
            if SORT_FROM <= n + T_AHEAD + 1 < NPAIR and a0 == 0 and n % 2 == 0:
                sort_words(n + T_AHEAD + 1)
            nc.vector.tensor_tensor(
                out=t12[:, 1].rearrange("p a h (i e) -> p a h i e", e=2),
                in0=tb[:, 1].rearrange("p a (i e) -> p a i e", e=2).unsqueeze(2).to_broadcast([P, na, 4, 32, 2]),
                in1=bank.rearrange("p (a h i e) -> p a h i e", a=na, h=4, e=2)[:, :, :, :, ::-1],
                op=ALU.mult,
            )

        def rope_q_add(n, eng, m0=0, m1=10):
            qo, i, grp, t12 = q_tile_of[n]
            if n < K_SHIFT:
                m0 = q_rows(n)[1]
                m1 = m0 + 8
            eng.tensor_tensor(
                out=qo[:, 10 * i + m0 : 10 * i + m1, 0:64], in0=t12[:, 0, m0:m1], in1=t12[:, 1, m0:m1], op=ALU.add
            )

        def store_q_tile(n, a):
            qo = q_tile_of[n][0]
            b, j = n // 4, 2 * (n % 4) + a
            dst = out_0[b].rearrange("(p j) h d -> p (j h d)", j=TPP)
            nc.sync.dma_start(
                out=dst[:, j * 512 : (j + 1) * 512],
                in_=qo[:, 2 + 4 * a : 6 + 4 * a, :].rearrange("p m d -> p (m d)"),
            )

        def rope_k_mul(n):
            if n + K_SHIFT < NPAIR:
                rk = q_rows(n + K_SHIFT)[2]
                t12 = q_tile_of[n + K_SHIFT][3][:, :, rk : rk + 2, :]
            else:
                rope_tmp[n] = rope.tile([P, 2, 2, 64], F32, name="t12k", tag="t12k", bufs=4)
                t12 = rope_tmp[n][:]
            bank = banks_of[n][2][:]
            nc.vector.tensor_tensor(
                out=t12[:, 0],
                in0=tab[:, n % 4, 0],
                in1=bank.rearrange("p (a s f) -> p a s f", a=2, s=4)[:, :, 0, :],
                op=ALU.mult,
            )
            nc.vector.tensor_tensor(
                out=t12[:, 1].rearrange("p a (i e) -> p a i e", e=2),
                in0=tab[:, n % 4, 1].rearrange("p a (i e) -> p a i e", e=2),
                in1=bank.rearrange("p (a s i e) -> p a s i e", a=2, s=4, e=2)[:, :, 0, :, ::-1],
                op=ALU.mult,
            )

        def rope_k_add(n, eng):
            ko, vo, k, grp = kv_tile_of[n]
            t12 = rope_tmp[n]
            eng.tensor_tensor(
                out=ko[:, 2 * k : 2 * k + 2, 0:64],
                in0=t12[:, 0],
                in1=t12[:, 1],
                op=ALU.add,
            )

        def copy_q(n):
            r0, rq, rk = q_rows(n)
            nc.scalar.copy(
                out=q_tile_of[n][0][:, r0 + rq : r0 + rq + 8, 64:128], in_=banks_of[n][1][:].rearrange("p (m f) -> p m f", m=8)
            )

        def copy_kv(n):
            bank_k = banks_of[n][2]
            ko, vo, k, grp = kv_tile_of[n]
            copy = nc.vector.tensor_copy if n <= KV_VECTOR_TO else nc.scalar.copy
            nc.scalar.copy(
                out=vo[:, 2 * k : 2 * k + 2, :], in_=bank_k[:].rearrange("p (a s f) -> p a s f", a=2, s=2)[:, :, 1, :]
            )
            if ko is None:
                r0, rq, rk = q_rows(n + K_SHIFT)
                ko, k = q_tile_of[n + K_SHIFT][0], (r0 + rk) // 2
            copy(
                out=ko[:, 2 * k : 2 * k + 2, 64:128],
                in_=bank_k[:].rearrange("p (a s f) -> p a s f", a=2, s=4)[:, :, 1, :],
            )

        def store_q(n):
            qo, i, grp, t12 = q_tile_of[n]
            if grp[-1] != n:
                return
            b, j0 = grp[0] // 4, 2 * (grp[0] % 4)
            dst = out_0[b].rearrange("(p j) h d -> p (j h d)", j=TPP)
            nc.sync.dma_start(
                out=dst[:, j0 * 512 : (j0 + 2 * len(grp)) * 512],
                in_=qo[:, 2 : 2 + 8 * len(grp), :].rearrange("p m d -> p (m d)"),
            )

        def store_k_beside_q(n):
            qo, i, grp, t12 = q_tile_of[n]
            if grp[-1] != n or n < K_SHIFT:
                return
            j = grp[0] - K_SHIFT
            b, j0 = j // 4, 2 * (j % 4)
            dst = out_1[b].rearrange("(p j) o d -> p (j o d)", j=TPP)[:, j0 * P : (j0 + 2 * len(grp)) * P]
            src = qo[:].rearrange("p (u m) d -> p u (m d)", m=2)
            nc.sync.dma_start(
                out=dst.rearrange("p (u x) -> p u x", u=len(grp)), in_=src[:, 0:10:9, :] if len(grp) == 2 else src[:, 0:1, :]
            )

        def store_kv(n, which):
            grp = kv_tile_of[n][3]
            if grp[-1] != n:
                return
            b, j0 = grp[0] // 4, 2 * (grp[0] % 4)
            dst = (out_1, out_2)[which][b].rearrange("(p j) o d -> p (j o d)", j=TPP)
            nc.sync.dma_start(
                out=dst[:, j0 * P : (j0 + 2 * len(grp)) * P],
                in_=kv_tile_of[n][which][:].rearrange("p m d -> p (m d)"),
            )

        def ahead(n):
            if n < NPAIR:
                xg_of[n] = evacuate(transposes(n))

        def kv_passes(j, tag="bank_k"):
            kv_out_tiles(j)
            bank_k = psum.tile([P, 512], F32, name="bank_k", tag=tag, bufs=(2 if tag == "bank_k" else 1))
            banks_of[j] = banks_of[j][:2] + (bank_k,)
            mx(j, bank_k, 512)
            if j > KV_VECTOR_TO:
                rope_k_mul(j)
                copy_kv(j)
            else:
                copy_kv(j)
                rope_k_mul(j)
            store_kv(j, 1)

        last = NPAIR - 1
        for n in range(NPAIR):
            j = n - K_LAG
            if n < K_SHIFT:
                q_out_tile(n)
            bank_r = psum.tile([P, 512], F32, name="bank_r", tag="bank_r")
            bank_p = psum.tile([P, 512], F32, name="bank_p", tag="bank_p")
            banks_of[n] = (bank_r, bank_p)
            mx(n, bank_r, 0)
            if n < FINE_FROM:
                rope_q_mul(n)
                rope_q_add(n, nc.gpsimd)
            else:
                for a in range(2):
                    rope_q_mul(n, a, 1)
                    if a == 0 and n + 2 < NPAIR:
                        xq_of[n + 2] = quantise_x(xg_of[n + 2])
                    rope_q_add(n, nc.gpsimd, 6 * a, 6 + 4 * a)
            if n == 0:
                ahead(2)
            mx(n, bank_p, 256)
            copy_q(n)
            ahead(n + T_AHEAD)
            if n < FINE_FROM and n + 2 < NPAIR:
                xq_of[n + 2] = quantise_x(xg_of[n + 2])
            if n == 1:
                quantise_w(0, 512, 768)
                quantise_w(1, 512, 768)
            if K_SHIFT <= n + 1 < NPAIR:
                q_out_tile(n + 1)
            if j >= 0:
                kv_passes(j)
            if n < FINE_FROM:
                store_q(n)
                store_k_beside_q(n)
            else:
                store_q_tile(n, 0)
                store_k_beside_q(n)
                store_q_tile(n, 1)
        kv_passes(last - 2)
        rope_k_add(last - 3, nc.gpsimd)
        rope_k_add(last - 2, nc.gpsimd)
        store_kv(last - 2, 0)
        kv_passes(last - 1, "tp0")
        kv_passes(last, "tp1")
        rope_k_add(last - 1, nc.vector)
        rope_k_add(last, nc.vector)
        store_kv(last, 0)
